import numpy as np
import ml_dtypes


def mxq(x, axis, fmt="e4m3"):
    dtype, down = {"e4m3": (ml_dtypes.float8_e4m3fn, 7), "e5m2": (ml_dtypes.float8_e5m2, 14)}[fmt]
    v = np.moveaxis(np.asarray(x, np.float32).astype(ml_dtypes.bfloat16).astype(np.float64), axis, -1)
    blocks = v.reshape(v.shape[:-1] + (-1, 32))
    amax = np.abs(blocks).max(-1, keepdims=True)
    byte = np.maximum(np.where(amax > 0, np.frexp(amax)[1] - 1 + 127, 0) - down, 1)
    scale = np.exp2(byte - 127.0)
    codes = (blocks / scale).astype(np.float32).astype(dtype).astype(np.float64)
    return np.moveaxis((codes * scale).reshape(v.shape), -1, axis)


WIDE = False


def mx_kscale(k):
    if not WIDE:
        return np.ones(k)
    levels = np.array([10, -10, 5, -5, 0])
    if k % 512:
        return np.exp2(np.random.permutation(np.resize(levels, k // 32))).repeat(32)
    a = np.empty((k // 512, 16))
    for p in range(k // 512):
        a[p, :8] = np.random.permutation(np.resize(levels, 8))
        for g in range(8):
            far = levels[np.abs(levels - a[p, g]) >= 10]
            a[p, g + 8] = far[np.random.randint(len(far))]
    return np.exp2(a.ravel()).repeat(32)


BF16 = ml_dtypes.bfloat16


def bf(x):
    return np.asarray(x, np.float32).astype(BF16)


def f64(x):
    return np.asarray(x).astype(np.float64)


B, IMG, P0, P1, C, F = 2, 512, 8, 16, 2, 512
E0, E1 = IMG // P0, IMG // P1
N0, N1 = E0 * E0, E1 * E1
D0, D1 = P0 * P0 * C, P1 * P1 * C


def setup_inputs():
    s = mx_kscale(D1)
    flat = np.random.standard_normal((B, N1, D1)) * s
    img = flat.reshape(B, E1, E1, P1, P1, C).transpose(0, 1, 3, 2, 4, 5).reshape(B, IMG, IMG, C)
    encoded = img.reshape(B, E0, P0, E0, P0, C).transpose(0, 1, 3, 2, 4, 5).reshape(B, N0, D0)
    return {"encoded": bf(encoded),
            "W": bf(np.random.standard_normal((D1, F)) / np.sqrt(D1) / s[:, None]),
            "b": bf(np.random.standard_normal(F) * 0.3),
            "pos_emb": bf(np.random.standard_normal((N1, F)) * 0.5)}


def core(encoded, W, b, pos_emb):
    x = f64(encoded).reshape(-1, E0, E0, P0, P0, C)
    img = x.transpose(0, 1, 3, 2, 4, 5).reshape(-1, IMG, IMG, C)
    new_patches = img.reshape(-1, E1, P1, E1, P1, C).transpose(0, 1, 3, 2, 4, 5)
    flat = new_patches.reshape(-1, N1, D1)
    return (mxq(flat, 2, "e4m3") @ mxq(f64(W), 0, "e4m3")) + f64(b) + f64(pos_emb)


def e4m3fn_bytes(y):
    return np.clip(np.asarray(y, np.float64), -448.0, 448.0).astype(np.float32).astype(ml_dtypes.float8_e4m3fn).view(np.uint8)


def reference(encoded, W, b, pos_emb):
    out = core(encoded, W, b, pos_emb)
    s = np.max(np.abs(out)) / 448.0
    return out, e4m3fn_bytes(out / s)

@@ -1,0 +1,208 @@
+from contextlib import ExitStack
+
+import concourse.mybir as mybir
+from concourse.masks import make_identity
+
+F32 = mybir.dt.float32
+BF16 = mybir.dt.bfloat16
+U32 = mybir.dt.uint32
+U8 = mybir.dt.uint8
+FP8X4 = mybir.dt.float8_e4m3fn_x4
+FP8 = mybir.dt.float8_e4m3fn
+ALU = mybir.AluOpType
+ACT = mybir.ActivationFunctionType
+AX = mybir.AxisListType
+
+P = 128
+F = 512
+XL = 8
+NPAIR = 8
+FLOPS = 2 * 2048 * 512 * 512
+
+CHUNKS = [(0, 0, 2), (0, 2, 2), (0, 4, 4), (1, 0, 4), (1, 4, 4)]
+CHUNK_OF_PAIR = {0: 0, 1: 1, 2: 2, 4: 3, 6: 4}
+POS_PIECES = [(0, 2), (2, 2), (4, 4)]
+CASTS = [(0, "v"), (2, "s"), (1, "v"), (3, "v"), (5, "s"), (4, "v"), (6, "v"), (7, "v")]
+
+
+def tile_resampling_kernel(tc, encoded, W, b, pos_emb, out_0, out_1):
+    nc = tc.nc
+    with ExitStack() as ctx:
+        const = ctx.enter_context(tc.tile_pool(name="const", bufs=1))
+        keep = ctx.enter_context(tc.tile_pool(name="keep", bufs=1))
+        work = ctx.enter_context(tc.tile_pool(name="work", bufs=3))
+        ps_t = ctx.enter_context(tc.psum_pool(name="ps_t", bufs=2))
+        ps_m = ctx.enter_context(tc.psum_pool(name="ps_m", bufs=4))
+        ps_x = ctx.enter_context(tc.psum_pool(name="ps_x", bufs=1))
+        ctx.enter_context(tc.manual_schedule())
+
+        enc_v = encoded.rearrange("i (y a xh r) d -> i xh y a (r d)", y=32, a=2, xh=4, r=16)
+        pos_v = pos_emb.rearrange("(p l) f -> p l f", l=XL)
+
+        b_row = const.tile([P, F], BF16, name="b_row")
+        nc.gpsimd.memset(b_row[:], 0.0)
+        nc.scalar.dma_start(out=b_row[0:1, :], in_=b.rearrange("(o f) -> o f", o=1))
+        ones = const.tile([P, P], BF16, name="ones")
+        nc.gpsimd.memset(ones[:], 1.0)
+        zero = const.tile([P, 1], F32, name="zero")
+        nc.gpsimd.memset(zero[:], 0.0)
+        ident = const.tile([P, P], F32, name="ident")
+        make_identity(nc, ident[:])
+        warm = const.tile([P, 1], F32, name="warm")
+        nc.scalar.activation(out=warm[:], in_=zero[:], func=ACT.Identity, bias=zero[:, 0:1], scale=zero[:, 0:1])
+
+        xraw = {}
+
+        def load_chunk(c):
+            i, l0, nl = CHUNKS[c]
+            t = keep.tile([P, 2, nl * 256], BF16, name="xraw%d" % c)
+            for xh in range(4):
+                nc.sync.dma_start(out=t[xh:P:4, :, :], in_=enc_v[i, xh, :, :, l0 * 256:(l0 + nl) * 256])
+            xraw[c] = t
+
+        pos_sb = {}
+
+        def load_pos(k):
+            l0, nl = POS_PIECES[k]
+            t = const.tile([P, nl, F], BF16, name="pos%d" % k)
+            nc.sync.dma_start(out=t[:], in_=pos_v[:, l0:l0 + nl, :])
+            for l in range(nl):
+                pos_sb[l0 + l] = t[:, l, :]
+
+        load_chunk(0)
+        w_raw = const.tile([P, 4, F], BF16, name="w_raw")
+        nc.sync.dma_start(out=w_raw[:], in_=W.rearrange("(p j) f -> p j f", j=4))
+        load_pos(0)
+        load_chunk(1)
+        load_pos(1)
+        load_chunk(2)
+        load_pos(2)
+        load_chunk(3)
+        load_chunk(4)
+
+        xr = {}
+        state = {}
+        o_sb = {}
+        posb = {}
+        stats = const.tile([P, NPAIR + 1], F32, name="stats")
+
+        def reorder(c):
+            i, l0, nl = CHUNKS[c]
+            t = keep.tile([P, nl, 256], F32, name="xr%d" % c)
+            src = xraw[c][:].bitcast(F32).rearrange("p a (l b ry h) -> p a l b ry h", l=nl, b=2, ry=8, h=8)
+            dst = t[:].rearrange("p l (a ry b h) -> p l a ry b h", a=2, ry=8, b=2, h=8)
+            for a in range(2):
+                for bb in range(2):
+                    nc.scalar.copy(out=dst[:, :, a, :, bb, :], in_=src[:, a, :, bb, :, :])
+            for l in range(nl):
+                xr[(i, l0 + l)] = t[:, l, :]
+
+        def transposes(j):
+            i, l0 = j // 4, 2 * (j % 4)
+            tp = ps_t.tile([P, 2, 2, P], F32, name="tp")
+            for tl in range(2):
+                for u in range(2):
+                    nc.tensor.transpose(out=tp[:, tl, u, :], in_=xr[(i, l0 + tl)][:, u:256:2], identity=ident[:])
+            xg = work.tile([P, 1024], BF16, name="xg", align_bytes=64)
+            nc.scalar.copy(out=xg[:].bitcast(F32).rearrange("p (tl n u) -> p tl n u", tl=2, u=2),
+                           in_=tp[:].rearrange("p tl u n -> p tl n u"))
+            state[("xg", j)] = xg
+
+        def quantise(j):
+            xc = work.tile([P, 256], U32, name="xc", align_bytes=64)
+            xs = work.tile([P, 256], U8, name="xs", align_bytes=64)
+            nc.vector.quantize_mx(out=xc[:].bitcast(FP8X4), scales=xs[:], in_=state[("xg", j)][:])
+            state[("xc", j)] = (xc, xs)
+
+        def multiply(j):
+            xc, xs = state[("xc", j)]
+            for tl in range(2):
+                acc = ps_m.tile([P, F], F32, name="acc")
+                nc.tensor.matmul_mx(out=acc[:], lhsT=xc[:, tl * P:(tl + 1) * P].bitcast(FP8X4),
+                                    lhsT_scale=xs[:, tl * P:(tl + 1) * P],
+                                    rhs=w_codes[:].bitcast(FP8X4), rhs_scale=w_scales[:],
+                                    start=True, stop=True)
+                state[("acc", j, tl)] = acc
+
+        def add_pos(j):
+            i, l0 = j // 4, 2 * (j % 4)
+            o = keep.tile([P, 2, F], F32, name="o%d" % j)
+            o_sb[j] = o
+            for tl in range(2):
+                nc.vector.tensor_tensor(out=o[:, tl, :], in0=state[("acc", j, tl)][:], in1=posb[l0 + tl][:],
+                                        op=ALU.add)
+            nc.sync.dma_start(out=out_0[i].rearrange("(p l) f -> p l f", l=XL)[:, l0:l0 + 2, :], in_=o[:])
+
+        def make_posb(l):
+            pb = const.tile([P, F], F32, name="posb%d" % l)
+            nc.gpsimd.tensor_tensor(out=pb[:], in0=pos_sb[l], in1=b_all[:], op=ALU.add)
+            posb[l] = pb
+
+        reorder(0)
+        b_ps = ps_x.tile([P, F], F32, name="b_ps")
+        nc.tensor.matmul(out=b_ps[:], lhsT=ones[:], rhs=b_row[:], start=True, stop=True)
+        b_all = const.tile([P, F], F32, name="b_all")
+        nc.scalar.copy(out=b_all[:], in_=b_ps[:])
+        for l in range(XL):
+            make_posb(l)
+        transposes(0)
+
+        w_grp = const.tile([P, F, 4], BF16, name="w_grp", align_bytes=64)
+        nc.vector.tensor_copy(out=w_grp[:], in_=w_raw[:].rearrange("p j f -> p f j"))
+        w_codes = const.tile([P, F], U32, name="w_codes", align_bytes=64)
+        w_scales = const.tile([P, F], U8, name="w_scales", align_bytes=64)
+        nc.vector.quantize_mx(out=w_codes[:].bitcast(FP8X4), scales=w_scales[:],
+                              in_=w_grp[:].rearrange("p f j -> p (f j)"))
+
+        reorder(1)
+        transposes(1)
+        quantise(0)
+        multiply(0)
+
+        for j in range(NPAIR):
+            if j + 2 < NPAIR:
+                if j + 2 in CHUNK_OF_PAIR:
+                    reorder(CHUNK_OF_PAIR[j + 2])
+                transposes(j + 2)
+            add_pos(j)
+            if j + 1 < NPAIR:
+                quantise(j + 1)
+                multiply(j + 1)
+                nc.vector.tensor_reduce(out=stats[:, j:j + 1], in_=o_sb[j][:].rearrange("p l f -> p (l f)"),
+                                        axis=AX.X, op=ALU.max, apply_absolute_value=True)
+            else:
+                for tl in range(2):
+                    nc.vector.tensor_reduce(out=stats[:, j + tl:j + tl + 1], in_=o_sb[j][:, tl, :],
+                                            axis=AX.X, op=ALU.max, apply_absolute_value=True)
+
+        pmax = const.tile([P, 1], F32, name="pmax")
+        nc.vector.tensor_reduce(out=pmax[:], in_=stats[:], axis=AX.X, op=ALU.max)
+        am_ps = ps_x.tile([P, P], F32, name="am_ps")
+        nc.tensor.transpose(out=am_ps[:], in_=pmax[:, 0:1].to_broadcast([P, P]), identity=ident[:])
+        amax = const.tile([P, 1], F32, name="amax")
+        nc.vector.tensor_reduce(out=amax[:], in_=am_ps[:], axis=AX.X, op=ALU.max)
+        rec = const.tile([P, 1], F32, name="rec")
+        nc.vector.reciprocal(out=rec[:], in_=amax[:])
+        fac = const.tile([P, 1], F32, name="fac")
+        nc.vector.tensor_scalar(out=fac[:], in0=rec[:], scalar1=448.0, scalar2=None, op0=ALU.mult)
+
+        q_sb = {}
+        done = {}
+        for hh in range(4):
+            q_sb[hh] = keep.tile([P, 2048], FP8, name="q%d" % hh)
+            done[hh] = 0
+        for j, eng in CASTS:
+            hh, jj = j // 2, j % 2
+            src = o_sb[j][:].rearrange("p l f -> p (l f)")
+            dst = q_sb[hh][:, jj * 1024:(jj + 1) * 1024]
+            if eng == "v":
+                nc.vector.tensor_scalar(out=dst, in0=src, scalar1=fac[:, 0:1], scalar2=None,
+                                        op0=ALU.mult, saturate=False)
+            else:
+                nc.scalar.activation(out=dst, in_=src, func=ACT.Identity, bias=zero[:, 0:1],
+                                     scale=fac[:, 0:1], saturate=False)
+            done[hh] += 1
+            if done[hh] == 2:
+                i, c0 = hh // 2, (hh % 2) * 2048
+                nc.sync.dma_start(out=out_1[i].rearrange("(p l) f -> p (l f)", l=XL)[:, c0:c0 + 2048],
+                                  in_=q_sb[hh][:].bitcast(U8))

@@ -16,13 +16,15 @@ AX = mybir.AxisListType
 P = 128
 F = 512
 XL = 8
-NPAIR = 8
 FLOPS = 2 * 2048 * 512 * 512
 
-CHUNKS = [(0, 0, 2), (0, 2, 2), (0, 4, 4), (1, 0, 4), (1, 4, 4)]
-CHUNK_OF_PAIR = {0: 0, 1: 1, 2: 2, 4: 3, 6: 4}
+CHUNKS = [(0, 0, 2), (0, 2, 6), (1, 0, 4), (1, 4, 4)]
+RGROUPS = [(0, 0, 2), (1, 0, 2), (1, 2, 4), (2, 0, 4), (3, 0, 4)]
 POS_PIECES = [(0, 2), (2, 2), (4, 4)]
-CASTS = [(0, "v"), (2, "s"), (1, "v"), (3, "v"), (5, "s"), (4, "v"), (6, "v"), (7, "v")]
+QGROUPS = [[0], [1], [2, 3], [4, 5], [6, 7]]
+W_SPLIT = 352
+CASTS = [(0, 0, 1024, "v"), (2, 0, 1024, "s"), (1, 0, 1024, "v"), (3, 0, 1024, "v"), (5, 0, 1024, "s"),
+         (4, 0, 1024, "v"), (6, 0, 1024, "v"), (7, 512, 512, "s"), (7, 0, 512, "v")]
 
 
 def tile_resampling_kernel(tc, encoded, W, b, pos_emb, out_0, out_1):
@@ -30,9 +32,8 @@ def tile_resampling_kernel(tc, encoded, W, b, pos_emb, out_0, out_1):
     with ExitStack() as ctx:
         const = ctx.enter_context(tc.tile_pool(name="const", bufs=1))
         keep = ctx.enter_context(tc.tile_pool(name="keep", bufs=1))
-        work = ctx.enter_context(tc.tile_pool(name="work", bufs=3))
         ps_t = ctx.enter_context(tc.psum_pool(name="ps_t", bufs=2))
-        ps_m = ctx.enter_context(tc.psum_pool(name="ps_m", bufs=4))
+        ps_m = ctx.enter_context(tc.psum_pool(name="ps_m", bufs=5))
         ps_x = ctx.enter_context(tc.psum_pool(name="ps_x", bufs=1))
         ctx.enter_context(tc.manual_schedule())
 
@@ -75,27 +76,40 @@ def tile_resampling_kernel(tc, encoded, W, b, pos_emb, out_0, out_1):
         load_pos(0)
         load_chunk(1)
         load_pos(1)
-        load_chunk(2)
         load_pos(2)
+        load_chunk(2)
         load_chunk(3)
-        load_chunk(4)
 
         xr = {}
-        state = {}
+        tp_of = {}
+        xg_of = {}
+        xc_of = {}
+        acc_of = {}
+        tmp_of = {}
         o_sb = {}
         posb = {}
-        stats = const.tile([P, NPAIR + 1], F32, name="stats")
+        stats = const.tile([P, 16], F32, name="stats")
+        n_stats = [0]
+        for g, pairs in enumerate(QGROUPS):
+            t = keep.tile([P, 1024 * len(pairs)], BF16, name="xg%d" % g, align_bytes=64)
+            for k, j in enumerate(pairs):
+                xg_of[j] = (t, k)
+        for j in range(8):
+            o_sb[j] = keep.tile([P, 2, F], F32, name="o%d" % j)
 
-        def reorder(c):
-            i, l0, nl = CHUNKS[c]
-            t = keep.tile([P, nl, 256], F32, name="xr%d" % c)
-            src = xraw[c][:].bitcast(F32).rearrange("p a (l b ry h) -> p a l b ry h", l=nl, b=2, ry=8, h=8)
-            dst = t[:].rearrange("p l (a ry b h) -> p l a ry b h", a=2, ry=8, b=2, h=8)
+        def reorder(g, eng):
+            c, k0, nl = RGROUPS[g]
+            i, l0, cl = CHUNKS[c]
+            t = keep.tile([P, nl, 256], F32, name="xr%d" % g)
+            src = xraw[c][:].bitcast(F32).rearrange("p a (l b ry h) -> p a l ry b h", l=cl, b=2, ry=8, h=8)
+            dst = t[:].rearrange("p l (a ry b h) -> p a l ry b h", a=2, ry=8, b=2, h=8)
             for a in range(2):
-                for bb in range(2):
-                    nc.scalar.copy(out=dst[:, :, a, :, bb, :], in_=src[:, a, :, bb, :, :])
+                if eng == "v":
+                    nc.vector.tensor_copy(out=dst[:, a], in_=src[:, a, k0:k0 + nl])
+                else:
+                    nc.scalar.copy(out=dst[:, a], in_=src[:, a, k0:k0 + nl])
             for l in range(nl):
-                xr[(i, l0 + l)] = t[:, l, :]
+                xr[(i, l0 + k0 + l)] = t[:, l, :]
 
         def transposes(j):
             i, l0 = j // 4, 2 * (j % 4)
@@ -103,81 +117,155 @@ def tile_resampling_kernel(tc, encoded, W, b, pos_emb, out_0, out_1):
             for tl in range(2):
                 for u in range(2):
                     nc.tensor.transpose(out=tp[:, tl, u, :], in_=xr[(i, l0 + tl)][:, u:256:2], identity=ident[:])
-            xg = work.tile([P, 1024], BF16, name="xg", align_bytes=64)
-            nc.scalar.copy(out=xg[:].bitcast(F32).rearrange("p (tl n u) -> p tl n u", tl=2, u=2),
-                           in_=tp[:].rearrange("p tl u n -> p tl n u"))
-            state[("xg", j)] = xg
+            tp_of[j] = tp
 
-        def quantise(j):
-            xc = work.tile([P, 256], U32, name="xc", align_bytes=64)
-            xs = work.tile([P, 256], U8, name="xs", align_bytes=64)
-            nc.vector.quantize_mx(out=xc[:].bitcast(FP8X4), scales=xs[:], in_=state[("xg", j)][:])
-            state[("xc", j)] = (xc, xs)
+        def evacuate(j):
+            t, k = xg_of[j]
+            nc.scalar.copy(out=t[:, k * 1024:(k + 1) * 1024].bitcast(F32).rearrange("p (tl n u) -> p tl n u", tl=2, u=2),
+                           in_=tp_of[j][:].rearrange("p tl u n -> p tl n u"))
 
-        def multiply(j):
-            xc, xs = state[("xc", j)]
-            for tl in range(2):
-                acc = ps_m.tile([P, F], F32, name="acc")
-                nc.tensor.matmul_mx(out=acc[:], lhsT=xc[:, tl * P:(tl + 1) * P].bitcast(FP8X4),
-                                    lhsT_scale=xs[:, tl * P:(tl + 1) * P],
-                                    rhs=w_codes[:].bitcast(FP8X4), rhs_scale=w_scales[:],
-                                    start=True, stop=True)
-                state[("acc", j, tl)] = acc
+        def quantise(g):
+            pairs = QGROUPS[g]
+            n = len(pairs)
+            xc = keep.tile([P, 256 * n], U32, name="xc%d" % g, align_bytes=64)
+            xs = keep.tile([P, 256 * n], U8, name="xs%d" % g, align_bytes=64)
+            nc.vector.quantize_mx(out=xc[:].bitcast(FP8X4), scales=xs[:], in_=xg_of[pairs[0]][0][:])
+            for k, j in enumerate(pairs):
+                for tl in range(2):
+                    xc_of[2 * j + tl] = (xc, xs, (2 * k + tl) * P)
 
-        def add_pos(j):
+        def multiply(t):
+            xc, xs, c0 = xc_of[t]
+            acc = ps_m.tile([P, F], F32, name="acc")
+            nc.tensor.matmul_mx(out=acc[:], lhsT=xc[:, c0:c0 + P].bitcast(FP8X4), lhsT_scale=xs[:, c0:c0 + P],
+                                rhs=w_codes[:].bitcast(FP8X4), rhs_scale=w_scales[:], start=True, stop=True)
+            acc_of[t] = acc
+
+        def add_vector(t):
+            nc.vector.tensor_tensor(out=o_sb[t // 2][:, t % 2, :], in0=acc_of[t][:], in1=posb[t % 8][:], op=ALU.add)
+
+        def out_of_psum(t):
+            tmp = keep.tile([P, F], F32, name="tmp%d" % t)
+            nc.scalar.copy(out=tmp[:], in_=acc_of[t][:])
+            tmp_of[t] = tmp
+
+        def add_gpsimd(t):
+            nc.gpsimd.tensor_tensor(out=o_sb[t // 2][:, t % 2, :], in0=tmp_of[t][:], in1=posb[t % 8][:], op=ALU.add)
+
+        def store(j):
             i, l0 = j // 4, 2 * (j % 4)
-            o = keep.tile([P, 2, F], F32, name="o%d" % j)
-            o_sb[j] = o
-            for tl in range(2):
-                nc.vector.tensor_tensor(out=o[:, tl, :], in0=state[("acc", j, tl)][:], in1=posb[l0 + tl][:],
-                                        op=ALU.add)
-            nc.sync.dma_start(out=out_0[i].rearrange("(p l) f -> p l f", l=XL)[:, l0:l0 + 2, :], in_=o[:])
+            nc.sync.dma_start(out=out_0[i].rearrange("(p l) f -> p l f", l=XL)[:, l0:l0 + 2, :], in_=o_sb[j][:])
+
+        def absmax(j, tl0, ntl):
+            k = n_stats[0]
+            n_stats[0] = k + 1
+            nc.vector.tensor_reduce(out=stats[:, k:k + 1],
+                                    in_=o_sb[j][:, tl0:tl0 + ntl, :].rearrange("p l f -> p (l f)"),
+                                    axis=AX.X, op=ALU.max, apply_absolute_value=True)
 
         def make_posb(l):
             pb = const.tile([P, F], F32, name="posb%d" % l)
             nc.gpsimd.tensor_tensor(out=pb[:], in0=pos_sb[l], in1=b_all[:], op=ALU.add)
             posb[l] = pb
 
-        reorder(0)
-        b_ps = ps_x.tile([P, F], F32, name="b_ps")
+        reorder(0, "v")
+        b_ps = ps_x.tile([P, F], F32, name="b_ps", tag="misc")
         nc.tensor.matmul(out=b_ps[:], lhsT=ones[:], rhs=b_row[:], start=True, stop=True)
-        b_all = const.tile([P, F], F32, name="b_all")
+        b_all = const.tile([P, F], BF16, name="b_all")
         nc.scalar.copy(out=b_all[:], in_=b_ps[:])
         for l in range(XL):
             make_posb(l)
         transposes(0)
 
         w_grp = const.tile([P, F, 4], BF16, name="w_grp", align_bytes=64)
-        nc.vector.tensor_copy(out=w_grp[:], in_=w_raw[:].rearrange("p j f -> p f j"))
+        nc.scalar.copy(out=w_grp[:, W_SPLIT:F, :], in_=w_raw[:, :, W_SPLIT:F].rearrange("p j f -> p f j"))
+        nc.vector.tensor_copy(out=w_grp[:, 0:W_SPLIT, :], in_=w_raw[:, :, 0:W_SPLIT].rearrange("p j f -> p f j"))
+        evacuate(0)
         w_codes = const.tile([P, F], U32, name="w_codes", align_bytes=64)
         w_scales = const.tile([P, F], U8, name="w_scales", align_bytes=64)
         nc.vector.quantize_mx(out=w_codes[:].bitcast(FP8X4), scales=w_scales[:],
                               in_=w_grp[:].rearrange("p f j -> p (f j)"))
-
-        reorder(1)
+        reorder(1, "s")
         transposes(1)
+        evacuate(1)
         quantise(0)
         multiply(0)
+        multiply(1)
 
-        for j in range(NPAIR):
-            if j + 2 < NPAIR:
-                if j + 2 in CHUNK_OF_PAIR:
-                    reorder(CHUNK_OF_PAIR[j + 2])
-                transposes(j + 2)
-            add_pos(j)
-            if j + 1 < NPAIR:
-                quantise(j + 1)
-                multiply(j + 1)
-                nc.vector.tensor_reduce(out=stats[:, j:j + 1], in_=o_sb[j][:].rearrange("p l f -> p (l f)"),
-                                        axis=AX.X, op=ALU.max, apply_absolute_value=True)
-            else:
-                for tl in range(2):
-                    nc.vector.tensor_reduce(out=stats[:, j + tl:j + tl + 1], in_=o_sb[j][:, tl, :],
-                                            axis=AX.X, op=ALU.max, apply_absolute_value=True)
+        reorder(2, "s")
+        transposes(2)
+        evacuate(2)
+        transposes(3)
+        evacuate(3)
+
+        add_vector(0)
+        add_vector(1)
+        store(0)
+        quantise(1)
+        multiply(2)
+        multiply(3)
+        absmax(0, 0, 2)
+
+        reorder(3, "s")
+        transposes(4)
+        evacuate(4)
+        transposes(5)
+        evacuate(5)
+
+        add_vector(2)
+        add_vector(3)
+        store(1)
+        quantise(2)
+        for t in (4, 5, 6, 7):
+            multiply(t)
+        absmax(1, 0, 2)
+
+        reorder(4, "s")
+        transposes(6)
+        evacuate(6)
+        transposes(7)
+        evacuate(7)
+
+        add_vector(4)
+        add_vector(5)
+        store(2)
+        quantise(3)
+        for t in (8, 9, 10):
+            multiply(t)
+        out_of_psum(9)
+        add_gpsimd(9)
+        absmax(2, 0, 2)
+
+        add_vector(8)
+        add_vector(6)
+        multiply(11)
+        out_of_psum(11)
+        add_gpsimd(11)
+        add_vector(10)
+        add_vector(7)
+        store(3)
+        quantise(4)
+        for t in (12, 13, 14, 15):
+            multiply(t)
+        for t in (12, 13, 14):
+            out_of_psum(t)
+            add_gpsimd(t)
+        absmax(3, 0, 2)
+
+        add_vector(15)
+        absmax(4, 0, 2)
+        store(4)
+        absmax(5, 0, 2)
+        store(5)
+        absmax(7, 1, 1)
+        absmax(6, 0, 2)
+        store(6)
+        absmax(7, 0, 1)
+        store(7)
 
         pmax = const.tile([P, 1], F32, name="pmax")
-        nc.vector.tensor_reduce(out=pmax[:], in_=stats[:], axis=AX.X, op=ALU.max)
-        am_ps = ps_x.tile([P, P], F32, name="am_ps")
+        nc.vector.tensor_reduce(out=pmax[:], in_=stats[:, 0:n_stats[0]], axis=AX.X, op=ALU.max)
+        am_ps = ps_x.tile([P, P], F32, name="am_ps", tag="misc")
         nc.tensor.transpose(out=am_ps[:], in_=pmax[:, 0:1].to_broadcast([P, P]), identity=ident[:])
         amax = const.tile([P, 1], F32, name="amax")
         nc.vector.tensor_reduce(out=amax[:], in_=am_ps[:], axis=AX.X, op=ALU.max)
@@ -191,18 +279,18 @@ def tile_resampling_kernel(tc, encoded, W, b, pos_emb, out_0, out_1):
         for hh in range(4):
             q_sb[hh] = keep.tile([P, 2048], FP8, name="q%d" % hh)
             done[hh] = 0
-        for j, eng in CASTS:
+        for j, c0, n, eng in CASTS:
             hh, jj = j // 2, j % 2
-            src = o_sb[j][:].rearrange("p l f -> p (l f)")
-            dst = q_sb[hh][:, jj * 1024:(jj + 1) * 1024]
+            src = o_sb[j][:].rearrange("p l f -> p (l f)")[:, c0:c0 + n]
+            dst = q_sb[hh][:, jj * 1024 + c0:jj * 1024 + c0 + n]
             if eng == "v":
                 nc.vector.tensor_scalar(out=dst, in0=src, scalar1=fac[:, 0:1], scalar2=None,
                                         op0=ALU.mult, saturate=False)
             else:
                 nc.scalar.activation(out=dst, in_=src, func=ACT.Identity, bias=zero[:, 0:1],
                                      scale=fac[:, 0:1], saturate=False)
-            done[hh] += 1
-            if done[hh] == 2:
-                i, c0 = hh // 2, (hh % 2) * 2048
-                nc.sync.dma_start(out=out_1[i].rearrange("(p l) f -> p (l f)", l=XL)[:, c0:c0 + 2048],
+            done[hh] += n
+            if done[hh] == 2048:
+                i, d0 = hh // 2, (hh % 2) * 2048
+                nc.sync.dma_start(out=out_1[i].rearrange("(p l) f -> p (l f)", l=XL)[:, d0:d0 + 2048],
                                   in_=q_sb[hh][:].bitcast(U8))

@@ -18,13 +18,10 @@ F = 512
 XL = 8
 FLOPS = 2 * 2048 * 512 * 512
 
-CHUNKS = [(0, 0, 2), (0, 2, 6), (1, 0, 4), (1, 4, 4)]
-RGROUPS = [(0, 0, 2), (1, 0, 2), (1, 2, 4), (2, 0, 4), (3, 0, 4)]
 POS_PIECES = [(0, 2), (2, 2), (4, 4)]
-QGROUPS = [[0], [1], [2, 3], [4, 5], [6, 7]]
-W_SPLIT = 352
-CASTS = [(0, 0, 1024, "v"), (2, 0, 1024, "s"), (1, 0, 1024, "v"), (3, 0, 1024, "v"), (5, 0, 1024, "s"),
-         (4, 0, 1024, "v"), (6, 0, 1024, "v"), (7, 512, 512, "s"), (7, 0, 512, "v")]
+RGROUPS = [(0, 0, 1), (0, 1, 1), (0, 2, 2), (1, 0, 4), (2, 0, 4), (3, 0, 4)]
+UNITS = [[0],[1],[2,3],[4,5],[6,7],[8,9],[10,11],[12,13],[14,15]]
+QGROUPS = [[0],[1],[2,3],[4,5,6,7],[8,9,10,11],[12,13,14,15]]
 
 
 def tile_resampling_kernel(tc, encoded, W, b, pos_emb, out_0, out_1):
@@ -41,103 +38,100 @@ def tile_resampling_kernel(tc, encoded, W, b, pos_emb, out_0, out_1):
         pos_v = pos_emb.rearrange("(p l) f -> p l f", l=XL)
 
         b_row = const.tile([P, F], BF16, name="b_row")
-        nc.gpsimd.memset(b_row[:], 0.0)
-        nc.scalar.dma_start(out=b_row[0:1, :], in_=b.rearrange("(o f) -> o f", o=1))
         ones = const.tile([P, P], BF16, name="ones")
-        nc.gpsimd.memset(ones[:], 1.0)
         zero = const.tile([P, 1], F32, name="zero")
-        nc.gpsimd.memset(zero[:], 0.0)
         ident = const.tile([P, P], F32, name="ident")
-        make_identity(nc, ident[:])
         warm = const.tile([P, 1], F32, name="warm")
-        nc.scalar.activation(out=warm[:], in_=zero[:], func=ACT.Identity, bias=zero[:, 0:1], scale=zero[:, 0:1])
-
+        w_raw = const.tile([P, 4, F], BF16, name="w_raw")
+        w_grp = const.tile([P, F, 4], BF16, name="w_grp", align_bytes=64)
+        w_codes = const.tile([P, F], U32, name="w_codes", align_bytes=64)
+        w_scales = const.tile([P, F], U8, name="w_scales", align_bytes=64)
+        b_all = const.tile([P, F], BF16, name="b_all")
+        stats = const.tile([P, 16], F32, name="stats")
+        pmax = const.tile([P, 1], F32, name="pmax")
+        amax = const.tile([P, 1], F32, name="amax")
+        rec = const.tile([P, 1], F32, name="rec")
+        fac = const.tile([P, 1], F32, name="fac")
         xraw = {}
-
-        def load_chunk(c):
-            i, l0, nl = CHUNKS[c]
-            t = keep.tile([P, 2, nl * 256], BF16, name="xraw%d" % c)
-            for xh in range(4):
-                nc.sync.dma_start(out=t[xh:P:4, :, :], in_=enc_v[i, xh, :, :, l0 * 256:(l0 + nl) * 256])
-            xraw[c] = t
-
+        for c in range(4):
+            xraw[c] = keep.tile([P, 2, 1024], BF16, name="xraw%d" % c)
         pos_sb = {}
+        pos_t = {}
+        for k, (l0, nl) in enumerate(POS_PIECES):
+            pos_t[k] = const.tile([P, nl, F], BF16, name="pos%d" % k)
+            for l in range(nl):
+                pos_sb[l0 + l] = pos_t[k][:, l, :]
+        posb = {}
+        for l in range(XL):
+            posb[l] = const.tile([P, F], F32, name="posb%d" % l)
+        xr = {}
+        xr_t = {}
+        for g, (c, k0, nl) in enumerate(RGROUPS):
+            xr_t[g] = keep.tile([P, nl, 256], F32, name="xr%d" % g)
+            for k in range(nl):
+                xr[4 * c + k0 + k] = xr_t[g][:, k, :]
+        xg_of = {}
+        xq_of = {}
+        xg_t = {}
+        xc_t = {}
+        xs_t = {}
+        for g, tiles in enumerate(QGROUPS):
+            xg_t[g] = keep.tile([P, 512 * len(tiles)], BF16, name="xg%d" % g, align_bytes=64)
+            xc_t[g] = keep.tile([P, P * len(tiles)], U32, name="xc%d" % g, align_bytes=64)
+            xs_t[g] = keep.tile([P, P * len(tiles)], U8, name="xs%d" % g, align_bytes=64)
+            for k, t in enumerate(tiles):
+                xg_of[t] = (g, k)
+        o_sb = {}
+        for j in range(8):
+            o_sb[j] = keep.tile([P, 2, F], F32, name="o%d" % j)
+        q_sb = {}
+        for j in range(8):
+            q_sb[j] = keep.tile([P, 1024], FP8, name="q%d" % j)
+        tp_of = {}
+        acc_of = {}
+        tmp_of = {}
+        n_stats = [0]
+
+        def load_chunk(c, xh):
+            i, l0 = c // 2, 4 * (c % 2)
+            nc.sync.dma_start(out=xraw[c][xh:P:4, :, :], in_=enc_v[i, xh, :, :, l0 * 256:(l0 + 4) * 256])
 
         def load_pos(k):
             l0, nl = POS_PIECES[k]
-            t = const.tile([P, nl, F], BF16, name="pos%d" % k)
-            nc.sync.dma_start(out=t[:], in_=pos_v[:, l0:l0 + nl, :])
-            for l in range(nl):
-                pos_sb[l0 + l] = t[:, l, :]
+            nc.sync.dma_start(out=pos_t[k][:], in_=pos_v[:, l0:l0 + nl, :])
 
-        load_chunk(0)
-        w_raw = const.tile([P, 4, F], BF16, name="w_raw")
-        nc.sync.dma_start(out=w_raw[:], in_=W.rearrange("(p j) f -> p j f", j=4))
-        load_pos(0)
-        load_chunk(1)
-        load_pos(1)
-        load_pos(2)
-        load_chunk(2)
-        load_chunk(3)
-
-        xr = {}
-        tp_of = {}
-        xg_of = {}
-        xc_of = {}
-        acc_of = {}
-        tmp_of = {}
-        o_sb = {}
-        posb = {}
-        stats = const.tile([P, 16], F32, name="stats")
-        n_stats = [0]
-        for g, pairs in enumerate(QGROUPS):
-            t = keep.tile([P, 1024 * len(pairs)], BF16, name="xg%d" % g, align_bytes=64)
-            for k, j in enumerate(pairs):
-                xg_of[j] = (t, k)
-        for j in range(8):
-            o_sb[j] = keep.tile([P, 2, F], F32, name="o%d" % j)
-
-        def reorder(g, eng):
+        def reorder(g, a, eng):
             c, k0, nl = RGROUPS[g]
-            i, l0, cl = CHUNKS[c]
-            t = keep.tile([P, nl, 256], F32, name="xr%d" % g)
-            src = xraw[c][:].bitcast(F32).rearrange("p a (l b ry h) -> p a l ry b h", l=cl, b=2, ry=8, h=8)
-            dst = t[:].rearrange("p l (a ry b h) -> p a l ry b h", a=2, ry=8, b=2, h=8)
-            for a in range(2):
-                if eng == "v":
-                    nc.vector.tensor_copy(out=dst[:, a], in_=src[:, a, k0:k0 + nl])
-                else:
-                    nc.scalar.copy(out=dst[:, a], in_=src[:, a, k0:k0 + nl])
-            for l in range(nl):
-                xr[(i, l0 + k0 + l)] = t[:, l, :]
+            src = xraw[c][:].bitcast(F32).rearrange("p a (l b ry h) -> p a l ry b h", l=4, b=2, ry=8, h=8)
+            dst = xr_t[g][:].rearrange("p l (a ry b h) -> p a l ry b h", a=2, ry=8, b=2, h=8)
+            if eng == "v":
+                nc.vector.tensor_copy(out=dst[:, a], in_=src[:, a, k0:k0 + nl])
+            else:
+                nc.scalar.copy(out=dst[:, a], in_=src[:, a, k0:k0 + nl])
 
-        def transposes(j):
-            i, l0 = j // 4, 2 * (j % 4)
-            tp = ps_t.tile([P, 2, 2, P], F32, name="tp")
-            for tl in range(2):
-                for u in range(2):
-                    nc.tensor.transpose(out=tp[:, tl, u, :], in_=xr[(i, l0 + tl)][:, u:256:2], identity=ident[:])
-            tp_of[j] = tp
+        def transposes(u):
+            tiles = UNITS[u]
+            tp = ps_t.tile([P, len(tiles), 2, P], F32, name="tp")
+            for k, t in enumerate(tiles):
+                for w in range(2):
+                    nc.tensor.transpose(out=tp[:, k, w, :], in_=xr[t][:, w:256:2], identity=ident[:])
+            tp_of[u] = tp
 
-        def evacuate(j):
-            t, k = xg_of[j]
-            nc.scalar.copy(out=t[:, k * 1024:(k + 1) * 1024].bitcast(F32).rearrange("p (tl n u) -> p tl n u", tl=2, u=2),
-                           in_=tp_of[j][:].rearrange("p tl u n -> p tl n u"))
+        def evacuate(u):
+            tiles = UNITS[u]
+            g, k = xg_of[tiles[0]]
+            n = len(tiles)
+            nc.scalar.copy(out=xg_t[g][:, k * 512:(k + n) * 512].bitcast(F32).rearrange("p (tl n w) -> p tl n w", tl=n, w=2),
+                           in_=tp_of[u][:].rearrange("p tl w n -> p tl n w"))
 
         def quantise(g):
-            pairs = QGROUPS[g]
-            n = len(pairs)
-            xc = keep.tile([P, 256 * n], U32, name="xc%d" % g, align_bytes=64)
-            xs = keep.tile([P, 256 * n], U8, name="xs%d" % g, align_bytes=64)
-            nc.vector.quantize_mx(out=xc[:].bitcast(FP8X4), scales=xs[:], in_=xg_of[pairs[0]][0][:])
-            for k, j in enumerate(pairs):
-                for tl in range(2):
-                    xc_of[2 * j + tl] = (xc, xs, (2 * k + tl) * P)
+            nc.vector.quantize_mx(out=xc_t[g][:].bitcast(FP8X4), scales=xs_t[g][:], in_=xg_t[g][:])
 
         def multiply(t):
-            xc, xs, c0 = xc_of[t]
+            g, k = xg_of[t]
             acc = ps_m.tile([P, F], F32, name="acc")
-            nc.tensor.matmul_mx(out=acc[:], lhsT=xc[:, c0:c0 + P].bitcast(FP8X4), lhsT_scale=xs[:, c0:c0 + P],
+            nc.tensor.matmul_mx(out=acc[:], lhsT=xc_t[g][:, k * P:(k + 1) * P].bitcast(FP8X4),
+                                lhsT_scale=xs_t[g][:, k * P:(k + 1) * P],
                                 rhs=w_codes[:].bitcast(FP8X4), rhs_scale=w_scales[:], start=True, stop=True)
             acc_of[t] = acc
 
@@ -156,141 +150,181 @@ def tile_resampling_kernel(tc, encoded, W, b, pos_emb, out_0, out_1):
             i, l0 = j // 4, 2 * (j % 4)
             nc.sync.dma_start(out=out_0[i].rearrange("(p l) f -> p l f", l=XL)[:, l0:l0 + 2, :], in_=o_sb[j][:])
 
-        def absmax(j, tl0, ntl):
+        def absmax(t, n):
             k = n_stats[0]
             n_stats[0] = k + 1
             nc.vector.tensor_reduce(out=stats[:, k:k + 1],
-                                    in_=o_sb[j][:, tl0:tl0 + ntl, :].rearrange("p l f -> p (l f)"),
+                                    in_=o_sb[t // 2][:, t % 2:t % 2 + n, :].rearrange("p l f -> p (l f)"),
                                     axis=AX.X, op=ALU.max, apply_absolute_value=True)
 
         def make_posb(l):
-            pb = const.tile([P, F], F32, name="posb%d" % l)
-            nc.gpsimd.tensor_tensor(out=pb[:], in0=pos_sb[l], in1=b_all[:], op=ALU.add)
-            posb[l] = pb
+            nc.gpsimd.tensor_tensor(out=posb[l][:], in0=pos_sb[l], in1=b_all[:], op=ALU.add)
 
-        reorder(0, "v")
-        b_ps = ps_x.tile([P, F], F32, name="b_ps", tag="misc")
-        nc.tensor.matmul(out=b_ps[:], lhsT=ones[:], rhs=b_row[:], start=True, stop=True)
-        b_all = const.tile([P, F], BF16, name="b_all")
-        nc.scalar.copy(out=b_all[:], in_=b_ps[:])
-        for l in range(XL):
-            make_posb(l)
-        transposes(0)
-
-        w_grp = const.tile([P, F, 4], BF16, name="w_grp", align_bytes=64)
-        nc.scalar.copy(out=w_grp[:, W_SPLIT:F, :], in_=w_raw[:, :, W_SPLIT:F].rearrange("p j f -> p f j"))
-        nc.vector.tensor_copy(out=w_grp[:, 0:W_SPLIT, :], in_=w_raw[:, :, 0:W_SPLIT].rearrange("p j f -> p f j"))
-        evacuate(0)
-        w_codes = const.tile([P, F], U32, name="w_codes", align_bytes=64)
-        w_scales = const.tile([P, F], U8, name="w_scales", align_bytes=64)
-        nc.vector.quantize_mx(out=w_codes[:].bitcast(FP8X4), scales=w_scales[:],
-                              in_=w_grp[:].rearrange("p f j -> p (f j)"))
-        reorder(1, "s")
-        transposes(1)
-        evacuate(1)
-        quantise(0)
-        multiply(0)
-        multiply(1)
-
-        reorder(2, "s")
-        transposes(2)
-        evacuate(2)
-        transposes(3)
-        evacuate(3)
-
-        add_vector(0)
-        add_vector(1)
-        store(0)
-        quantise(1)
-        multiply(2)
-        multiply(3)
-        absmax(0, 0, 2)
-
-        reorder(3, "s")
-        transposes(4)
-        evacuate(4)
-        transposes(5)
-        evacuate(5)
-
-        add_vector(2)
-        add_vector(3)
-        store(1)
-        quantise(2)
-        for t in (4, 5, 6, 7):
-            multiply(t)
-        absmax(1, 0, 2)
-
-        reorder(4, "s")
-        transposes(6)
-        evacuate(6)
-        transposes(7)
-        evacuate(7)
-
-        add_vector(4)
-        add_vector(5)
-        store(2)
-        quantise(3)
-        for t in (8, 9, 10):
-            multiply(t)
-        out_of_psum(9)
-        add_gpsimd(9)
-        absmax(2, 0, 2)
-
-        add_vector(8)
-        add_vector(6)
-        multiply(11)
-        out_of_psum(11)
-        add_gpsimd(11)
-        add_vector(10)
-        add_vector(7)
-        store(3)
-        quantise(4)
-        for t in (12, 13, 14, 15):
-            multiply(t)
-        for t in (12, 13, 14):
-            out_of_psum(t)
-            add_gpsimd(t)
-        absmax(3, 0, 2)
-
-        add_vector(15)
-        absmax(4, 0, 2)
-        store(4)
-        absmax(5, 0, 2)
-        store(5)
-        absmax(7, 1, 1)
-        absmax(6, 0, 2)
-        store(6)
-        absmax(7, 0, 1)
-        store(7)
-
-        pmax = const.tile([P, 1], F32, name="pmax")
-        nc.vector.tensor_reduce(out=pmax[:], in_=stats[:, 0:n_stats[0]], axis=AX.X, op=ALU.max)
-        am_ps = ps_x.tile([P, P], F32, name="am_ps", tag="misc")
-        nc.tensor.transpose(out=am_ps[:], in_=pmax[:, 0:1].to_broadcast([P, P]), identity=ident[:])
-        amax = const.tile([P, 1], F32, name="amax")
-        nc.vector.tensor_reduce(out=amax[:], in_=am_ps[:], axis=AX.X, op=ALU.max)
-        rec = const.tile([P, 1], F32, name="rec")
-        nc.vector.reciprocal(out=rec[:], in_=amax[:])
-        fac = const.tile([P, 1], F32, name="fac")
-        nc.vector.tensor_scalar(out=fac[:], in0=rec[:], scalar1=448.0, scalar2=None, op0=ALU.mult)
-
-        q_sb = {}
-        done = {}
-        for hh in range(4):
-            q_sb[hh] = keep.tile([P, 2048], FP8, name="q%d" % hh)
-            done[hh] = 0
-        for j, c0, n, eng in CASTS:
-            hh, jj = j // 2, j % 2
+        def cast(j, c0, n, eng):
             src = o_sb[j][:].rearrange("p l f -> p (l f)")[:, c0:c0 + n]
-            dst = q_sb[hh][:, jj * 1024 + c0:jj * 1024 + c0 + n]
+            dst = q_sb[j][:, c0:c0 + n]
             if eng == "v":
                 nc.vector.tensor_scalar(out=dst, in0=src, scalar1=fac[:, 0:1], scalar2=None,
                                         op0=ALU.mult, saturate=False)
             else:
                 nc.scalar.activation(out=dst, in_=src, func=ACT.Identity, bias=zero[:, 0:1],
                                      scale=fac[:, 0:1], saturate=False)
-            done[hh] += n
-            if done[hh] == 2048:
-                i, d0 = hh // 2, (hh % 2) * 2048
-                nc.sync.dma_start(out=out_1[i].rearrange("(p l) f -> p (l f)", l=XL)[:, d0:d0 + 2048],
-                                  in_=q_sb[hh][:].bitcast(U8))
+
+        def store_bytes(j):
+            i, d0 = j // 4, (j % 4) * 1024
+            nc.sync.dma_start(out=out_1[i].rearrange("(p l) f -> p (l f)", l=XL)[:, d0:d0 + 1024],
+                              in_=q_sb[j][:].bitcast(U8))
+
+        load_chunk(0, 0)
+        nc.gpsimd.memset(ones[:], 1.0)
+        load_chunk(0, 1)
+        load_chunk(0, 2)
+        nc.gpsimd.memset(zero[:], 0.0)
+        load_chunk(0, 3)
+        make_identity(nc, ident[:])
+        nc.sync.dma_start(out=w_raw[:], in_=W.rearrange("(p j) f -> p j f", j=4))
+        nc.vector.memset(b_row[:], 0.0)
+        nc.scalar.activation(out=warm[:], in_=zero[:], func=ACT.Identity, bias=zero[:, 0:1], scale=zero[:, 0:1])
+        nc.sync.dma_start(out=b_row[0:1, :], in_=b.rearrange("(o f) -> o f", o=1))
+        load_pos(0)
+        load_pos(1)
+        load_chunk(1, 0)
+        load_chunk(1, 1)
+        load_chunk(1, 2)
+        reorder(0, 0, "s")
+        load_chunk(1, 3)
+        reorder(0, 1, "s")
+        reorder(1, 0, "s")
+        transposes(0)
+        reorder(1, 1, "s")
+        reorder(2, 0, "s")
+        nc.vector.tensor_copy(out=w_grp[:], in_=w_raw[:].rearrange("p j f -> p f j"))
+        load_pos(2)
+        b_ps = ps_x.tile([P, F], F32, name="b_ps", tag="misc")
+        nc.tensor.matmul(out=b_ps[:], lhsT=ones[:], rhs=b_row[:], start=True, stop=True)
+        load_chunk(2, 0)
+        evacuate(0)
+        transposes(1)
+        load_chunk(2, 1)
+        nc.scalar.copy(out=b_all[:], in_=b_ps[:])
+        load_chunk(2, 2)
+        evacuate(1)
+        load_chunk(2, 3)
+        make_posb(0)
+        quantise(0)
+        reorder(2, 1, "s")
+        load_chunk(3, 0)
+        nc.vector.quantize_mx(out=w_codes[:].bitcast(FP8X4), scales=w_scales[:], in_=w_grp[:].rearrange("p f j -> p (f j)"))
+        load_chunk(3, 1)
+        reorder(3, 0, "s")
+        load_chunk(3, 2)
+        transposes(2)
+        quantise(1)
+        reorder(3, 1, "s")
+        make_posb(1)
+        multiply(0)
+        multiply(1)
+        evacuate(2)
+        add_vector(0)
+        transposes(3)
+        load_chunk(3, 3)
+        make_posb(2)
+        quantise(2)
+        transposes(4)
+        add_vector(1)
+        evacuate(3)
+        absmax(0, 2)
+        reorder(4, 0, "s")
+        multiply(2)
+        store(0)
+        make_posb(3)
+        multiply(3)
+        evacuate(4)
+        add_vector(2)
+        reorder(4, 1, "s")
+        quantise(3)
+        make_posb(4)
+        reorder(5, 0, "s")
+        transposes(5)
+        add_vector(3)
+        reorder(5, 1, "s")
+        absmax(2, 2)
+        multiply(4)
+        store(1)
+        make_posb(5)
+        evacuate(5)
+        multiply(5)
+        multiply(6)
+        multiply(7)
+        add_vector(4)
+        transposes(6)
+        out_of_psum(7)
+        make_posb(6)
+        add_vector(5)
+        transposes(7)
+        evacuate(6)
+        absmax(4, 2)
+        store(2)
+        make_posb(7)
+        transposes(8)
+        evacuate(7)
+        add_vector(6)
+        quantise(4)
+        evacuate(8)
+        add_gpsimd(7)
+        absmax(6, 1)
+        multiply(8)
+        multiply(9)
+        quantise(5)
+        out_of_psum(8)
+        multiply(10)
+        multiply(11)
+        store(3)
+        add_vector(10)
+        out_of_psum(9)
+        multiply(12)
+        add_gpsimd(8)
+        multiply(13)
+        absmax(7, 1)
+        out_of_psum(12)
+        multiply(14)
+        multiply(15)
+        add_vector(11)
+        out_of_psum(13)
+        add_gpsimd(9)
+        absmax(10, 2)
+        store(5)
+        add_vector(14)
+        add_gpsimd(12)
+        store(4)
+        absmax(8, 2)
+        add_gpsimd(13)
+        add_vector(15)
+        absmax(14, 1)
+        store(7)
+        absmax(15, 1)
+        store(6)
+        absmax(12, 2)
+        nc.vector.tensor_reduce(out=pmax[:], in_=stats[:, 0:n_stats[0]], axis=AX.X, op=ALU.max)
+        am_ps = ps_x.tile([P, P], F32, name="am_ps", tag="misc")
+        nc.tensor.transpose(out=am_ps[:], in_=pmax[:, 0:1].to_broadcast([P, P]), identity=ident[:])
+        nc.vector.tensor_reduce(out=amax[:], in_=am_ps[:], axis=AX.X, op=ALU.max)
+        nc.vector.reciprocal(out=rec[:], in_=amax[:])
+        nc.vector.tensor_scalar(out=fac[:], in0=rec[:], scalar1=448.0, scalar2=None, op0=ALU.mult)
+        cast(0, 0, 1024, "v")
+        cast(2, 0, 1024, "s")
+        cast(1, 0, 1024, "v")
+        store_bytes(0)
+        cast(3, 0, 1024, "v")
+        store_bytes(1)
+        cast(5, 0, 1024, "s")
+        store_bytes(2)
+        cast(4, 0, 1024, "v")
+        store_bytes(3)
+        cast(6, 0, 1024, "v")
+        store_bytes(4)
+        cast(7, 512, 512, "s")
+        store_bytes(5)
+        cast(7, 0, 512, "v")
+        store_bytes(6)
+        store_bytes(7)

@@ -233,7 +233,8 @@ def tile_resampling_kernel(tc, encoded, W, b, pos_emb, out_0, out_1):
         transposes(4)
         add_vector(1)
         evacuate(3)
-        absmax(0, 2)
+        absmax(0, 1)
+        absmax(1, 1)
         reorder(4, 0, "s")
         multiply(2)
         store(0)
@@ -248,7 +249,8 @@ def tile_resampling_kernel(tc, encoded, W, b, pos_emb, out_0, out_1):
         transposes(5)
         add_vector(3)
         reorder(5, 1, "s")
-        absmax(2, 2)
+        absmax(2, 1)
+        absmax(3, 1)
         multiply(4)
         store(1)
         make_posb(5)
@@ -263,7 +265,8 @@ def tile_resampling_kernel(tc, encoded, W, b, pos_emb, out_0, out_1):
         add_vector(5)
         transposes(7)
         evacuate(6)
-        absmax(4, 2)
+        absmax(4, 1)
+        absmax(5, 1)
         store(2)
         make_posb(7)
         transposes(8)
@@ -292,7 +295,8 @@ def tile_resampling_kernel(tc, encoded, W, b, pos_emb, out_0, out_1):
         add_vector(11)
         out_of_psum(13)
         add_gpsimd(9)
-        absmax(10, 2)
+        absmax(10, 1)
+        absmax(11, 1)
         store(5)
         add_vector(14)
         add_gpsimd(12)

@@ -187,19 +187,18 @@ def tile_resampling_kernel(tc, encoded, W, b, pos_emb, out_0, out_1):
         nc.scalar.activation(out=warm[:], in_=zero[:], func=ACT.Identity, bias=zero[:, 0:1], scale=zero[:, 0:1])
         nc.sync.dma_start(out=b_row[0:1, :], in_=b.rearrange("(o f) -> o f", o=1))
         load_pos(0)
-        load_pos(1)
         load_chunk(1, 0)
         load_chunk(1, 1)
         load_chunk(1, 2)
         reorder(0, 0, "s")
         load_chunk(1, 3)
+        load_pos(1)
         reorder(0, 1, "s")
         reorder(1, 0, "s")
         transposes(0)
         reorder(1, 1, "s")
         reorder(2, 0, "s")
         nc.vector.tensor_copy(out=w_grp[:], in_=w_raw[:].rearrange("p j f -> p f j"))
-        load_pos(2)
         b_ps = ps_x.tile([P, F], F32, name="b_ps", tag="misc")
         nc.tensor.matmul(out=b_ps[:], lhsT=ones[:], rhs=b_row[:], start=True, stop=True)
         load_chunk(2, 0)
@@ -210,6 +209,7 @@ def tile_resampling_kernel(tc, encoded, W, b, pos_emb, out_0, out_1):
         load_chunk(2, 2)
         evacuate(1)
         load_chunk(2, 3)
+        load_pos(2)
         make_posb(0)
         quantise(0)
         reorder(2, 1, "s")

@@ -327,8 +327,7 @@ def tile_resampling_kernel(tc, encoded, W, b, pos_emb, out_0, out_1):
         store_bytes(3)
         cast(6, 0, 1024, "v")
         store_bytes(4)
-        cast(7, 512, 512, "s")
+        cast(7, 0, 1024, "s")
         store_bytes(5)
-        cast(7, 0, 512, "v")
         store_bytes(6)
         store_bytes(7)

@@ -19,9 +19,13 @@ XL = 8
 FLOPS = 2 * 2048 * 512 * 512
 
 POS_PIECES = [(0, 2), (2, 2), (4, 4)]
-RGROUPS = [(0, 0, 1), (0, 1, 1), (0, 2, 2), (1, 0, 4), (2, 0, 4), (3, 0, 4)]
-UNITS = [[0],[1],[2,3],[4,5],[6,7],[8,9],[10,11],[12,13],[14,15]]
-QGROUPS = [[0],[1],[2,3],[4,5,6,7],[8,9,10,11],[12,13,14,15]]
+CHUNKS = [(0, 0, 4), (1, 0, 4), (0, 4, 4), (1, 4, 4)]
+UNITS = [((u // 2) % 2, 4 * (u // 4) + 2 * (u % 2)) for u in range(8)]
+NU = len(UNITS)
+G_UNITS = [1, 2, 3, 4, 5, 6]
+POSB_BEFORE = {0: [2, 3], 1: [4]}
+POSB_AFTER = {2: [6], 3: [5], 4: [7]}
+W_SPLIT = 400
 
 
 def tile_resampling_kernel(tc, encoded, W, b, pos_emb, out_0, out_1):
@@ -49,12 +53,12 @@ def tile_resampling_kernel(tc, encoded, W, b, pos_emb, out_0, out_1):
         b_all = const.tile([P, F], BF16, name="b_all")
         stats = const.tile([P, 16], F32, name="stats")
         pmax = const.tile([P, 1], F32, name="pmax")
-        amax = const.tile([P, 1], F32, name="amax")
-        rec = const.tile([P, 1], F32, name="rec")
+        junk = const.tile([P, 3, P], F32, name="junk")
+        scale = const.tile([P, 1], F32, name="scale")
         fac = const.tile([P, 1], F32, name="fac")
-        xraw = {}
-        for c in range(4):
-            xraw[c] = keep.tile([P, 2, 1024], BF16, name="xraw%d" % c)
+        xraw = []
+        for c, (i, l0, nl) in enumerate(CHUNKS):
+            xraw.append(keep.tile([P, 2, nl * 256], BF16, name="xraw%d" % c))
         pos_sb = {}
         pos_t = {}
         for k, (l0, nl) in enumerate(POS_PIECES):
@@ -65,269 +69,241 @@ def tile_resampling_kernel(tc, encoded, W, b, pos_emb, out_0, out_1):
         for l in range(XL):
             posb[l] = const.tile([P, F], F32, name="posb%d" % l)
         xr = {}
-        xr_t = {}
-        for g, (c, k0, nl) in enumerate(RGROUPS):
-            xr_t[g] = keep.tile([P, nl, 256], F32, name="xr%d" % g)
-            for k in range(nl):
-                xr[4 * c + k0 + k] = xr_t[g][:, k, :]
-        xg_of = {}
-        xq_of = {}
-        xg_t = {}
-        xc_t = {}
-        xs_t = {}
-        for g, tiles in enumerate(QGROUPS):
-            xg_t[g] = keep.tile([P, 512 * len(tiles)], BF16, name="xg%d" % g, align_bytes=64)
-            xc_t[g] = keep.tile([P, P * len(tiles)], U32, name="xc%d" % g, align_bytes=64)
-            xs_t[g] = keep.tile([P, P * len(tiles)], U8, name="xs%d" % g, align_bytes=64)
-            for k, t in enumerate(tiles):
-                xg_of[t] = (g, k)
+        xr0 = [keep.tile([P, 256], F32, name="xr0a"), keep.tile([P, 256], F32, name="xr0b")]
+        xc0 = []
+        xs0 = []
+        xg0 = []
+        for k in range(2):
+            xg0.append(keep.tile([P, 512], BF16, name="xg0%d" % k, align_bytes=64))
+            xc0.append(keep.tile([P, P], U32, name="xc0%d" % k, align_bytes=64))
+            xs0.append(keep.tile([P, P], U8, name="xs0%d" % k, align_bytes=64))
+        for u in range(1, NU):
+            xr[u] = keep.tile([P, 2, 256], F32, name="xr%d" % u)
+        xg = {}
+        xc = {}
+        xs = {}
         o_sb = {}
-        for j in range(8):
-            o_sb[j] = keep.tile([P, 2, F], F32, name="o%d" % j)
         q_sb = {}
-        for j in range(8):
-            q_sb[j] = keep.tile([P, 1024], FP8, name="q%d" % j)
+        for u in range(NU):
+            xg[u] = keep.tile([P, 1024], BF16, name="xg%d" % u, align_bytes=64)
+            xc[u] = keep.tile([P, 256], U32, name="xc%d" % u, align_bytes=64)
+            xs[u] = keep.tile([P, 256], U8, name="xs%d" % u, align_bytes=64)
+            o_sb[u] = keep.tile([P, 2, F], F32, name="o%d" % u)
+            q_sb[u] = keep.tile([P, 1024], FP8, name="q%d" % u)
         tp_of = {}
         acc_of = {}
         tmp_of = {}
         n_stats = [0]
 
-        def load_chunk(c, xh):
-            i, l0 = c // 2, 4 * (c % 2)
-            nc.sync.dma_start(out=xraw[c][xh:P:4, :, :], in_=enc_v[i, xh, :, :, l0 * 256:(l0 + 4) * 256])
+        def load_chunk(c, xh, queue):
+            i, l0, nl = CHUNKS[c]
+            queue.dma_start(out=xraw[c][xh:P:4, :, :], in_=enc_v[i, xh, :, :, l0 * 256:(l0 + nl) * 256])
 
-        def load_pos(k):
+        def load_pos(k, queue):
             l0, nl = POS_PIECES[k]
-            nc.sync.dma_start(out=pos_t[k][:], in_=pos_v[:, l0:l0 + nl, :])
+            queue.dma_start(out=pos_t[k][:], in_=pos_v[:, l0:l0 + nl, :])
 
-        def reorder(g, a, eng):
-            c, k0, nl = RGROUPS[g]
-            src = xraw[c][:].bitcast(F32).rearrange("p a (l b ry h) -> p a l ry b h", l=4, b=2, ry=8, h=8)
-            dst = xr_t[g][:].rearrange("p l (a ry b h) -> p a l ry b h", a=2, ry=8, b=2, h=8)
-            if eng == "v":
-                nc.vector.tensor_copy(out=dst[:, a], in_=src[:, a, k0:k0 + nl])
-            else:
-                nc.scalar.copy(out=dst[:, a], in_=src[:, a, k0:k0 + nl])
+        def raw_words(u):
+            i, l0 = UNITS[u]
+            c = [i == ci and cl0 <= l0 < cl0 + nl for ci, cl0, nl in CHUNKS].index(True)
+            cl0, nl = CHUNKS[c][1], CHUNKS[c][2]
+            v = xraw[c][:].bitcast(F32).rearrange("p a (l s ry h) -> p a l ry s h", l=nl, s=2, ry=8, h=8)
+            return v[:, :, l0 - cl0:l0 - cl0 + 2]
+
+        def reorder_first(k, copy):
+            copy(out=xr0[k][:].rearrange("p (a ry s h) -> p a ry s h", a=2, ry=8, s=2, h=8),
+                 in_=raw_words(0)[:, :, k])
+
+        def reorder(u, a):
+            dst = xr[u][:].rearrange("p l (a ry s h) -> p a l ry s h", a=2, ry=8, s=2, h=8)
+            nc.scalar.copy(out=dst[:, a], in_=raw_words(u)[:, a])
+
+        def transposes_first(k):
+            tp = ps_t.tile([P, 2, 2, P], F32, name="tp")
+            for w in range(2):
+                nc.tensor.transpose(out=tp[:, 0, w, :], in_=xr0[k][:, w:256:2], identity=ident[:])
+            tp_of[0, k] = tp
+
+        def evacuate_first(k):
+            nc.scalar.copy(out=xg0[k][:].bitcast(F32).rearrange("p (n w) -> p n w", w=2),
+                           in_=tp_of[0, k][:, 0].rearrange("p w n -> p n w"))
+
+        def quantise_first(k):
+            nc.vector.quantize_mx(out=xc0[k][:].bitcast(FP8X4), scales=xs0[k][:], in_=xg0[k][:])
 
         def transposes(u):
-            tiles = UNITS[u]
-            tp = ps_t.tile([P, len(tiles), 2, P], F32, name="tp")
-            for k, t in enumerate(tiles):
+            tp = ps_t.tile([P, 2, 2, P], F32, name="tp")
+            for k in range(2):
                 for w in range(2):
-                    nc.tensor.transpose(out=tp[:, k, w, :], in_=xr[t][:, w:256:2], identity=ident[:])
+                    nc.tensor.transpose(out=tp[:, k, w, :], in_=xr[u][:, k, w:256:2], identity=ident[:])
             tp_of[u] = tp
 
         def evacuate(u):
-            tiles = UNITS[u]
-            g, k = xg_of[tiles[0]]
-            n = len(tiles)
-            nc.scalar.copy(out=xg_t[g][:, k * 512:(k + n) * 512].bitcast(F32).rearrange("p (tl n w) -> p tl n w", tl=n, w=2),
-                           in_=tp_of[u][:].rearrange("p tl w n -> p tl n w"))
+            nc.scalar.copy(out=xg[u][:].bitcast(F32).rearrange("p (k n w) -> p k n w", k=2, w=2),
+                           in_=tp_of[u][:].rearrange("p k w n -> p k n w"))
 
-        def quantise(g):
-            nc.vector.quantize_mx(out=xc_t[g][:].bitcast(FP8X4), scales=xs_t[g][:], in_=xg_t[g][:])
+        def quantise(u):
+            nc.vector.quantize_mx(out=xc[u][:].bitcast(FP8X4), scales=xs[u][:], in_=xg[u][:])
 
-        def multiply(t):
-            g, k = xg_of[t]
+        def multiply(u, k):
             acc = ps_m.tile([P, F], F32, name="acc")
-            nc.tensor.matmul_mx(out=acc[:], lhsT=xc_t[g][:, k * P:(k + 1) * P].bitcast(FP8X4),
-                                lhsT_scale=xs_t[g][:, k * P:(k + 1) * P],
+            codes = xc0[k][:] if u == 0 else xc[u][:, k * P:(k + 1) * P]
+            scales = xs0[k][:] if u == 0 else xs[u][:, k * P:(k + 1) * P]
+            nc.tensor.matmul_mx(out=acc[:], lhsT=codes.bitcast(FP8X4), lhsT_scale=scales,
                                 rhs=w_codes[:].bitcast(FP8X4), rhs_scale=w_scales[:], start=True, stop=True)
-            acc_of[t] = acc
+            acc_of[u, k] = acc
 
-        def add_vector(t):
-            nc.vector.tensor_tensor(out=o_sb[t // 2][:, t % 2, :], in0=acc_of[t][:], in1=posb[t % 8][:], op=ALU.add)
+        def add_vector(u, k):
+            nc.vector.tensor_tensor(out=o_sb[u][:, k, :], in0=acc_of[u, k][:], in1=posb[UNITS[u][1] + k][:], op=ALU.add)
 
-        def out_of_psum(t):
-            tmp = keep.tile([P, F], F32, name="tmp%d" % t)
-            nc.scalar.copy(out=tmp[:], in_=acc_of[t][:])
-            tmp_of[t] = tmp
+        def out_of_psum(u, k):
+            tmp = keep.tile([P, F], F32, name="tmp%d" % u)
+            nc.scalar.copy(out=tmp[:], in_=acc_of[u, k][:])
+            tmp_of[u, k] = tmp
 
-        def add_gpsimd(t):
-            nc.gpsimd.tensor_tensor(out=o_sb[t // 2][:, t % 2, :], in0=tmp_of[t][:], in1=posb[t % 8][:], op=ALU.add)
+        def add_gpsimd(u, k):
+            nc.gpsimd.tensor_tensor(out=o_sb[u][:, k, :], in0=tmp_of[u, k][:], in1=posb[UNITS[u][1] + k][:], op=ALU.add)
 
-        def store(j):
-            i, l0 = j // 4, 2 * (j % 4)
-            nc.sync.dma_start(out=out_0[i].rearrange("(p l) f -> p l f", l=XL)[:, l0:l0 + 2, :], in_=o_sb[j][:])
+        def store(u):
+            i, l0 = UNITS[u]
+            nc.sync.dma_start(out=out_0[i].rearrange("(p l) f -> p l f", l=XL)[:, l0:l0 + 2, :], in_=o_sb[u][:])
 
-        def absmax(t, n):
-            k = n_stats[0]
-            n_stats[0] = k + 1
-            nc.vector.tensor_reduce(out=stats[:, k:k + 1],
-                                    in_=o_sb[t // 2][:, t % 2:t % 2 + n, :].rearrange("p l f -> p (l f)"),
-                                    axis=AX.X, op=ALU.max, apply_absolute_value=True)
+        def absmax(u, k):
+            j = n_stats[0]
+            n_stats[0] = j + 1
+            nc.vector.tensor_reduce(out=stats[:, j:j + 1], in_=o_sb[u][:, k, :], axis=AX.X, op=ALU.max,
+                                    apply_absolute_value=True)
 
         def make_posb(l):
             nc.gpsimd.tensor_tensor(out=posb[l][:], in0=pos_sb[l], in1=b_all[:], op=ALU.add)
 
-        def cast(j, c0, n, eng):
-            src = o_sb[j][:].rearrange("p l f -> p (l f)")[:, c0:c0 + n]
-            dst = q_sb[j][:, c0:c0 + n]
+        def cast(u, eng):
+            src = o_sb[u][:].rearrange("p l f -> p (l f)")
             if eng == "v":
-                nc.vector.tensor_scalar(out=dst, in0=src, scalar1=fac[:, 0:1], scalar2=None,
+                nc.vector.tensor_scalar(out=q_sb[u][:], in0=src, scalar1=fac[:, 0:1], scalar2=None,
                                         op0=ALU.mult, saturate=False)
             else:
-                nc.scalar.activation(out=dst, in_=src, func=ACT.Identity, bias=zero[:, 0:1],
+                nc.scalar.activation(out=q_sb[u][:], in_=src, func=ACT.Identity, bias=zero[:, 0:1],
                                      scale=fac[:, 0:1], saturate=False)
 
-        def store_bytes(j):
-            i, d0 = j // 4, (j % 4) * 1024
-            nc.sync.dma_start(out=out_1[i].rearrange("(p l) f -> p (l f)", l=XL)[:, d0:d0 + 1024],
-                              in_=q_sb[j][:].bitcast(U8))
+        def store_bytes(u):
+            i, l0 = UNITS[u]
+            nc.sync.dma_start(out=out_1[i].rearrange("(p l) f -> p (l f)", l=XL)[:, l0 * F:(l0 + 2) * F],
+                              in_=q_sb[u][:].bitcast(U8))
 
-        load_chunk(0, 0)
+        nc.gpsimd.memset(b_row[:], 0.0)
         nc.gpsimd.memset(ones[:], 1.0)
-        load_chunk(0, 1)
-        load_chunk(0, 2)
         nc.gpsimd.memset(zero[:], 0.0)
-        load_chunk(0, 3)
-        make_identity(nc, ident[:])
-        nc.sync.dma_start(out=w_raw[:], in_=W.rearrange("(p j) f -> p j f", j=4))
-        nc.vector.memset(b_row[:], 0.0)
+        load_chunk(0, 3, nc.scalar)
         nc.scalar.activation(out=warm[:], in_=zero[:], func=ACT.Identity, bias=zero[:, 0:1], scale=zero[:, 0:1])
+        make_identity(nc, ident[:])
+        load_pos(1, nc.gpsimd)
+        load_chunk(0, 0, nc.sync)
+        load_chunk(0, 1, nc.sync)
+        load_chunk(0, 2, nc.sync)
         nc.sync.dma_start(out=b_row[0:1, :], in_=b.rearrange("(o f) -> o f", o=1))
-        load_pos(0)
-        load_chunk(1, 0)
-        load_chunk(1, 1)
-        load_chunk(1, 2)
-        reorder(0, 0, "s")
-        load_chunk(1, 3)
-        load_pos(1)
-        reorder(0, 1, "s")
-        reorder(1, 0, "s")
-        transposes(0)
-        reorder(1, 1, "s")
-        reorder(2, 0, "s")
-        nc.vector.tensor_copy(out=w_grp[:], in_=w_raw[:].rearrange("p j f -> p f j"))
+        nc.sync.dma_start(out=w_raw[:], in_=W.rearrange("(p j) f -> p j f", j=4))
+        load_pos(0, nc.sync)
+        for xh in range(4):
+            load_chunk(1, xh, nc.sync)
+        for xh in range(4):
+            load_chunk(2, xh, nc.sync)
+        for xh in range(4):
+            load_chunk(3, xh, nc.sync)
+        load_pos(2, nc.sync)
+
         b_ps = ps_x.tile([P, F], F32, name="b_ps", tag="misc")
+        reorder_first(0, nc.scalar.copy)
+        reorder_first(1, nc.vector.tensor_copy)
         nc.tensor.matmul(out=b_ps[:], lhsT=ones[:], rhs=b_row[:], start=True, stop=True)
-        load_chunk(2, 0)
-        evacuate(0)
-        transposes(1)
-        load_chunk(2, 1)
-        nc.scalar.copy(out=b_all[:], in_=b_ps[:])
-        load_chunk(2, 2)
-        evacuate(1)
-        load_chunk(2, 3)
-        load_pos(2)
-        make_posb(0)
-        quantise(0)
-        reorder(2, 1, "s")
-        load_chunk(3, 0)
+        transposes_first(0)
+        transposes_first(1)
+        reorder(1, 0)
+        reorder(1, 1)
+        w_view = w_raw[:].rearrange("p j f -> p f j")
+        nc.vector.tensor_copy(out=b_all[:], in_=b_ps[:])
+        nc.vector.tensor_copy(out=w_grp[:, 0:W_SPLIT, :], in_=w_view[:, 0:W_SPLIT, :])
+        evacuate_first(0)
+        nc.scalar.copy(out=w_grp[:, W_SPLIT:F, :], in_=w_view[:, W_SPLIT:F, :])
+        quantise_first(0)
+        evacuate_first(1)
         nc.vector.quantize_mx(out=w_codes[:].bitcast(FP8X4), scales=w_scales[:], in_=w_grp[:].rearrange("p f j -> p (f j)"))
-        load_chunk(3, 1)
-        reorder(3, 0, "s")
-        load_chunk(3, 2)
-        transposes(2)
-        quantise(1)
-        reorder(3, 1, "s")
+        quantise_first(1)
+        make_posb(0)
         make_posb(1)
-        multiply(0)
-        multiply(1)
-        evacuate(2)
-        add_vector(0)
-        transposes(3)
-        load_chunk(3, 3)
-        make_posb(2)
-        quantise(2)
-        transposes(4)
-        add_vector(1)
-        evacuate(3)
-        absmax(0, 1)
-        absmax(1, 1)
-        reorder(4, 0, "s")
-        multiply(2)
-        store(0)
-        make_posb(3)
-        multiply(3)
-        evacuate(4)
-        add_vector(2)
-        reorder(4, 1, "s")
-        quantise(3)
-        make_posb(4)
-        reorder(5, 0, "s")
-        transposes(5)
-        add_vector(3)
-        reorder(5, 1, "s")
-        absmax(2, 1)
-        absmax(3, 1)
-        multiply(4)
-        store(1)
-        make_posb(5)
-        evacuate(5)
-        multiply(5)
-        multiply(6)
-        multiply(7)
-        add_vector(4)
-        transposes(6)
-        out_of_psum(7)
-        make_posb(6)
-        add_vector(5)
-        transposes(7)
-        evacuate(6)
-        absmax(4, 1)
+        transposes(1)
+        multiply(0, 0)
+        multiply(0, 1)
+        evacuate(1)
+        quantise(1)
+        for u in (2, 3):
+            reorder(u, 0)
+            reorder(u, 1)
+
+        for u in range(NU):
+            g = u in G_UNITS
+            if g:
+                out_of_psum(u, 1)
+            if u + 2 < NU:
+                transposes(u + 2)
+            if u == 1:
+                quantise(2)
+            add_vector(u, 0)
+            if 1 < u < NU - 1:
+                quantise(u + 1)
+            if not g:
+                add_vector(u, 1)
+            if u + 1 < NU:
+                multiply(u + 1, 0)
+                multiply(u + 1, 1)
+            if u + 2 < NU:
+                evacuate(u + 2)
+            if u + 4 < NU:
+                reorder(u + 4, 0)
+                reorder(u + 4, 1)
+            for l in POSB_BEFORE.get(u, []):
+                make_posb(l)
+            if g:
+                add_gpsimd(u, 1)
+            for l in POSB_AFTER.get(u, []):
+                make_posb(l)
+            if not g:
+                store(u)
+            if u < NU - 1:
+                absmax(u, 0)
+            if not g and u < NU - 1:
+                absmax(u, 1)
+            if u - 2 in G_UNITS:
+                store(u - 2)
+                if u < NU - 1:
+                    absmax(u - 2, 1)
+        absmax(7, 0)
         absmax(5, 1)
-        store(2)
-        make_posb(7)
-        transposes(8)
-        evacuate(7)
-        add_vector(6)
-        quantise(4)
-        evacuate(8)
-        add_gpsimd(7)
-        absmax(6, 1)
-        multiply(8)
-        multiply(9)
-        quantise(5)
-        out_of_psum(8)
-        multiply(10)
-        multiply(11)
-        store(3)
-        add_vector(10)
-        out_of_psum(9)
-        multiply(12)
-        add_gpsimd(8)
-        multiply(13)
         absmax(7, 1)
-        out_of_psum(12)
-        multiply(14)
-        multiply(15)
-        add_vector(11)
-        out_of_psum(13)
-        add_gpsimd(9)
-        absmax(10, 1)
-        absmax(11, 1)
-        store(5)
-        add_vector(14)
-        add_gpsimd(12)
-        store(4)
-        absmax(8, 2)
-        add_gpsimd(13)
-        add_vector(15)
-        absmax(14, 1)
-        store(7)
-        absmax(15, 1)
+        n_early = n_stats[0] - 1
+        nc.vector.tensor_reduce(out=pmax[:], in_=stats[:, 0:n_early], axis=AX.X, op=ALU.max)
+        am_ps = ps_x.tile([P, 3, P], F32, name="am_ps", tag="misc")
+        nc.tensor.transpose(out=am_ps[:, 0, :], in_=stats[:, n_early:n_early + 1].to_broadcast([P, P]), identity=ident[:])
+        nc.tensor.transpose(out=am_ps[:, 1, :], in_=pmax[:, 0:1].to_broadcast([P, P]), identity=ident[:])
+        absmax(6, 1)
         store(6)
-        absmax(12, 2)
-        nc.vector.tensor_reduce(out=pmax[:], in_=stats[:, 0:n_stats[0]], axis=AX.X, op=ALU.max)
-        am_ps = ps_x.tile([P, P], F32, name="am_ps", tag="misc")
-        nc.tensor.transpose(out=am_ps[:], in_=pmax[:, 0:1].to_broadcast([P, P]), identity=ident[:])
-        nc.vector.tensor_reduce(out=amax[:], in_=am_ps[:], axis=AX.X, op=ALU.max)
-        nc.vector.reciprocal(out=rec[:], in_=amax[:])
-        nc.vector.tensor_scalar(out=fac[:], in0=rec[:], scalar1=448.0, scalar2=None, op0=ALU.mult)
-        cast(0, 0, 1024, "v")
-        cast(2, 0, 1024, "s")
-        cast(1, 0, 1024, "v")
+        nc.tensor.transpose(out=am_ps[:, 2, :], in_=stats[:, n_early + 1:n_early + 2].to_broadcast([P, P]), identity=ident[:])
+        nc.vector.tensor_scalar(out=junk[:], in0=am_ps[:], scalar1=1.0 / 448.0, scalar2=None, op0=ALU.mult,
+                                op1=ALU.max, accum_out=scale[:, 0:1])
+        nc.vector.reciprocal(out=fac[:], in_=scale[:])
+        cast(0, "v")
+        cast(2, "s")
+        cast(1, "v")
         store_bytes(0)
-        cast(3, 0, 1024, "v")
+        cast(3, "v")
         store_bytes(1)
-        cast(5, 0, 1024, "s")
+        cast(5, "s")
         store_bytes(2)
-        cast(4, 0, 1024, "v")
+        cast(4, "v")
         store_bytes(3)
-        cast(6, 0, 1024, "v")
+        cast(6, "v")
         store_bytes(4)
-        cast(7, 0, 1024, "s")
+        cast(7, "s")
         store_bytes(5)
         store_bytes(6)
         store_bytes(7)

@@ -22,9 +22,7 @@ POS_PIECES = [(0, 2), (2, 2), (4, 4)]
 CHUNKS = [(0, 0, 4), (1, 0, 4), (0, 4, 4), (1, 4, 4)]
 UNITS = [((u // 2) % 2, 4 * (u // 4) + 2 * (u % 2)) for u in range(8)]
 NU = len(UNITS)
-G_UNITS = [1, 2, 3, 4, 5, 6]
-POSB_BEFORE = {0: [2, 3], 1: [4]}
-POSB_AFTER = {2: [6], 3: [5], 4: [7]}
+QGROUPS = [[1], [2, 3], [4, 5], [6, 7]]
 W_SPLIT = 400
 
 
@@ -66,8 +64,9 @@ def tile_resampling_kernel(tc, encoded, W, b, pos_emb, out_0, out_1):
             for l in range(nl):
                 pos_sb[l0 + l] = pos_t[k][:, l, :]
         posb = {}
-        for l in range(XL):
-            posb[l] = const.tile([P, F], F32, name="posb%d" % l)
+        for l in (0, 1):
+            posb_v = const.tile([P, F], F32, name="posb%d" % l)
+            posb[l] = posb_v[:]
         xr = {}
         xr0 = [keep.tile([P, 256], F32, name="xr0a"), keep.tile([P, 256], F32, name="xr0b")]
         xc0 = []
@@ -84,11 +83,21 @@ def tile_resampling_kernel(tc, encoded, W, b, pos_emb, out_0, out_1):
         xs = {}
         o_sb = {}
         q_sb = {}
+        xg_t = {}
+        xc_t = {}
+        xs_t = {}
+        for g, units in enumerate(QGROUPS):
+            n = len(units)
+            xg_t[g] = keep.tile([P, 1024 * n], BF16, name="xg%d" % g, tag="slot%d" % g, align_bytes=64)
+            xc_t[g] = keep.tile([P, 256 * n], U32, name="xc%d" % g, align_bytes=64)
+            xs_t[g] = keep.tile([P, 256 * n], U8, name="xs%d" % g, align_bytes=64)
+            for k, u in enumerate(units):
+                xg[u] = xg_t[g][:, k * 1024:(k + 1) * 1024]
+                xc[u] = xc_t[g][:, k * 256:(k + 1) * 256]
+                xs[u] = xs_t[g][:, k * 256:(k + 1) * 256]
         for u in range(NU):
-            xg[u] = keep.tile([P, 1024], BF16, name="xg%d" % u, align_bytes=64)
-            xc[u] = keep.tile([P, 256], U32, name="xc%d" % u, align_bytes=64)
-            xs[u] = keep.tile([P, 256], U8, name="xs%d" % u, align_bytes=64)
-            o_sb[u] = keep.tile([P, 2, F], F32, name="o%d" % u)
+            if u != 4:
+                o_sb[u] = keep.tile([P, 2, F], F32, name="o%d" % u)
             q_sb[u] = keep.tile([P, 1024], FP8, name="q%d" % u)
         tp_of = {}
         acc_of = {}
@@ -139,11 +148,11 @@ def tile_resampling_kernel(tc, encoded, W, b, pos_emb, out_0, out_1):
             tp_of[u] = tp
 
         def evacuate(u):
-            nc.scalar.copy(out=xg[u][:].bitcast(F32).rearrange("p (k n w) -> p k n w", k=2, w=2),
+            nc.scalar.copy(out=xg[u].bitcast(F32).rearrange("p (k n w) -> p k n w", k=2, w=2),
                            in_=tp_of[u][:].rearrange("p k w n -> p k n w"))
 
-        def quantise(u):
-            nc.vector.quantize_mx(out=xc[u][:].bitcast(FP8X4), scales=xs[u][:], in_=xg[u][:])
+        def quantise(g):
+            nc.vector.quantize_mx(out=xc_t[g][:].bitcast(FP8X4), scales=xs_t[g][:], in_=xg_t[g][:])
 
         def multiply(u, k):
             acc = ps_m.tile([P, F], F32, name="acc")
@@ -154,15 +163,15 @@ def tile_resampling_kernel(tc, encoded, W, b, pos_emb, out_0, out_1):
             acc_of[u, k] = acc
 
         def add_vector(u, k):
-            nc.vector.tensor_tensor(out=o_sb[u][:, k, :], in0=acc_of[u, k][:], in1=posb[UNITS[u][1] + k][:], op=ALU.add)
+            nc.vector.tensor_tensor(out=o_sb[u][:, k, :], in0=acc_of[u, k][:], in1=posb[UNITS[u][1] + k], op=ALU.add)
 
         def out_of_psum(u, k):
-            tmp = keep.tile([P, F], F32, name="tmp%d" % u)
+            tmp = keep.tile([P, F], F32, name="tmp%d" % (2 * u + k))
             nc.scalar.copy(out=tmp[:], in_=acc_of[u, k][:])
             tmp_of[u, k] = tmp
 
         def add_gpsimd(u, k):
-            nc.gpsimd.tensor_tensor(out=o_sb[u][:, k, :], in0=tmp_of[u, k][:], in1=posb[UNITS[u][1] + k][:], op=ALU.add)
+            nc.gpsimd.tensor_tensor(out=o_sb[u][:, k, :], in0=tmp_of[u, k][:], in1=posb[UNITS[u][1] + k], op=ALU.add)
 
         def store(u):
             i, l0 = UNITS[u]
@@ -174,8 +183,16 @@ def tile_resampling_kernel(tc, encoded, W, b, pos_emb, out_0, out_1):
             nc.vector.tensor_reduce(out=stats[:, j:j + 1], in_=o_sb[u][:, k, :], axis=AX.X, op=ALU.max,
                                     apply_absolute_value=True)
 
+        def posb_tile(l, n, g):
+            t = keep.tile([P, n, F], F32, name="posb_%d" % l, tag="slot%d" % g, align_bytes=64)
+            for k in range(n):
+                posb[l + k] = t[:, k, :]
+
+        def make_posb_vector(l):
+            nc.vector.tensor_tensor(out=posb[l], in0=pos_sb[l], in1=b_ps[:], op=ALU.add)
+
         def make_posb(l):
-            nc.gpsimd.tensor_tensor(out=posb[l][:], in0=pos_sb[l], in1=b_all[:], op=ALU.add)
+            nc.gpsimd.tensor_tensor(out=posb[l], in0=pos_sb[l], in1=b_all[:], op=ALU.add)
 
         def cast(u, eng):
             src = o_sb[u][:].rearrange("p l f -> p (l f)")
@@ -229,63 +246,112 @@ def tile_resampling_kernel(tc, encoded, W, b, pos_emb, out_0, out_1):
         evacuate_first(1)
         nc.vector.quantize_mx(out=w_codes[:].bitcast(FP8X4), scales=w_scales[:], in_=w_grp[:].rearrange("p f j -> p (f j)"))
         quantise_first(1)
-        make_posb(0)
-        make_posb(1)
+        make_posb_vector(0)
+        make_posb_vector(1)
         transposes(1)
         multiply(0, 0)
         multiply(0, 1)
         evacuate(1)
-        quantise(1)
-        for u in (2, 3):
+        quantise(0)
+        posb_tile(2, 1, 0)
+        posb3 = const.tile([P, F], F32, name="posb3")
+        posb[3] = posb3[:]
+        make_posb(2)
+        make_posb(3)
+        for u in (2, 3, 4):
             reorder(u, 0)
             reorder(u, 1)
-
-        for u in range(NU):
-            g = u in G_UNITS
-            if g:
-                out_of_psum(u, 1)
-            if u + 2 < NU:
-                transposes(u + 2)
-            if u == 1:
-                quantise(2)
-            add_vector(u, 0)
-            if 1 < u < NU - 1:
-                quantise(u + 1)
-            if not g:
-                add_vector(u, 1)
-            if u + 1 < NU:
-                multiply(u + 1, 0)
-                multiply(u + 1, 1)
-            if u + 2 < NU:
-                evacuate(u + 2)
-            if u + 4 < NU:
-                reorder(u + 4, 0)
-                reorder(u + 4, 1)
-            for l in POSB_BEFORE.get(u, []):
-                make_posb(l)
-            if g:
-                add_gpsimd(u, 1)
-            for l in POSB_AFTER.get(u, []):
-                make_posb(l)
-            if not g:
-                store(u)
-            if u < NU - 1:
-                absmax(u, 0)
-            if not g and u < NU - 1:
-                absmax(u, 1)
-            if u - 2 in G_UNITS:
-                store(u - 2)
-                if u < NU - 1:
-                    absmax(u - 2, 1)
+        transposes(2)
+        transposes(3)
+        multiply(1, 0)
+        multiply(1, 1)
+        evacuate(2)
+        add_vector(0, 0)
+        add_vector(0, 1)
+        store(0)
+        absmax(0, 0)
+        absmax(0, 1)
+        evacuate(3)
+        reorder(5, 0)
+        reorder(5, 1)
+        transposes(4)
+        quantise(1)
+        add_vector(1, 0)
+        posb_tile(4, 2, 1)
+        make_posb(4)
+        make_posb(5)
+        transposes(5)
+        evacuate(4)
+        multiply(2, 0)
+        multiply(2, 1)
+        multiply(3, 0)
+        reorder(6, 0)
+        reorder(6, 1)
+        evacuate(5)
+        add_vector(1, 1)
+        store(1)
+        absmax(1, 0)
+        absmax(1, 1)
+        transposes(6)
+        reorder(7, 0)
+        reorder(7, 1)
+        quantise(2)
+        add_vector(2, 0)
+        posb_tile(6, 2, 2)
+        make_posb(6)
+        make_posb(7)
+        evacuate(6)
+        multiply(3, 1)
+        transposes(7)
+        add_vector(2, 1)
+        store(2)
+        absmax(2, 0)
+        absmax(2, 1)
+        evacuate(7)
+        add_vector(3, 0)
+        multiply(4, 0)
+        multiply(4, 1)
+        multiply(5, 0)
+        multiply(5, 1)
+        quantise(3)
+        o_sb[4] = keep.tile([P, 2, F], F32, name="o4", tag="slot3", align_bytes=64)
+        out_of_psum(4, 0)
+        add_gpsimd(4, 0)
+        out_of_psum(4, 1)
+        add_gpsimd(4, 1)
+        add_vector(3, 1)
+        store(3)
+        store(4)
+        absmax(3, 0)
+        absmax(3, 1)
+        out_of_psum(5, 0)
+        add_gpsimd(5, 0)
+        multiply(6, 0)
+        multiply(6, 1)
+        multiply(7, 0)
+        multiply(7, 1)
+        out_of_psum(5, 1)
+        add_gpsimd(5, 1)
+        out_of_psum(6, 0)
+        add_gpsimd(6, 0)
+        absmax(4, 0)
+        add_vector(6, 1)
+        absmax(4, 1)
+        add_vector(7, 0)
+        absmax(6, 1)
+        add_vector(7, 1)
+        store(7)
+        store(5)
         absmax(7, 0)
-        absmax(5, 1)
+        absmax(5, 0)
         absmax(7, 1)
+        absmax(5, 1)
         n_early = n_stats[0] - 1
         nc.vector.tensor_reduce(out=pmax[:], in_=stats[:, 0:n_early], axis=AX.X, op=ALU.max)
         am_ps = ps_x.tile([P, 3, P], F32, name="am_ps", tag="misc")
         nc.tensor.transpose(out=am_ps[:, 0, :], in_=stats[:, n_early:n_early + 1].to_broadcast([P, P]), identity=ident[:])
         nc.tensor.transpose(out=am_ps[:, 1, :], in_=pmax[:, 0:1].to_broadcast([P, P]), identity=ident[:])
-        absmax(6, 1)
+        absmax(6, 0)
         store(6)
         nc.tensor.transpose(out=am_ps[:, 2, :], in_=stats[:, n_early + 1:n_early + 2].to_broadcast([P, P]), identity=ident[:])
         nc.vector.tensor_scalar(out=junk[:], in0=am_ps[:], scalar1=1.0 / 448.0, scalar2=None, op0=ALU.mult,

@@ -18,7 +18,7 @@ F = 512
 XL = 8
 FLOPS = 2 * 2048 * 512 * 512
 
-POS_PIECES = [(0, 2), (2, 2), (4, 4)]
+POS_PIECES = [(0, 1), (1, 1), (2, 2), (4, 2), (6, 2)]
 CHUNKS = [(0, 0, 4), (1, 0, 4), (0, 4, 4), (1, 4, 4)]
 UNITS = [((u // 2) % 2, 4 * (u // 4) + 2 * (u % 2)) for u in range(8)]
 NU = len(UNITS)
@@ -214,7 +214,6 @@ def tile_resampling_kernel(tc, encoded, W, b, pos_emb, out_0, out_1):
         load_chunk(0, 3, nc.scalar)
         nc.scalar.activation(out=warm[:], in_=zero[:], func=ACT.Identity, bias=zero[:, 0:1], scale=zero[:, 0:1])
         make_identity(nc, ident[:])
-        load_pos(1, nc.gpsimd)
         load_chunk(0, 0, nc.sync)
         load_chunk(0, 1, nc.sync)
         load_chunk(0, 2, nc.sync)
@@ -223,11 +222,14 @@ def tile_resampling_kernel(tc, encoded, W, b, pos_emb, out_0, out_1):
         load_pos(0, nc.sync)
         for xh in range(4):
             load_chunk(1, xh, nc.sync)
+        load_pos(1, nc.sync)
+        load_pos(2, nc.sync)
         for xh in range(4):
             load_chunk(2, xh, nc.sync)
+        load_pos(3, nc.sync)
         for xh in range(4):
             load_chunk(3, xh, nc.sync)
-        load_pos(2, nc.sync)
+        load_pos(4, nc.sync)
 
         b_ps = ps_x.tile([P, F], F32, name="b_ps", tag="misc")
         reorder_first(0, nc.scalar.copy)
@@ -254,11 +256,13 @@ def tile_resampling_kernel(tc, encoded, W, b, pos_emb, out_0, out_1):
         evacuate(1)
         quantise(0)
         posb_tile(2, 1, 0)
-        posb3 = const.tile([P, F], F32, name="posb3")
-        posb[3] = posb3[:]
+        for l in (3, 4):
+            posb_g = const.tile([P, F], F32, name="posb%d" % l)
+            posb[l] = posb_g[:]
         make_posb(2)
         make_posb(3)
-        for u in (2, 3, 4):
+        make_posb(4)
+        for u in (2, 3):
             reorder(u, 0)
             reorder(u, 1)
         transposes(2)
@@ -272,43 +276,45 @@ def tile_resampling_kernel(tc, encoded, W, b, pos_emb, out_0, out_1):
         absmax(0, 0)
         absmax(0, 1)
         evacuate(3)
-        reorder(5, 0)
-        reorder(5, 1)
+        for u in (4, 5):
+            reorder(u, 0)
+            reorder(u, 1)
         transposes(4)
-        quantise(1)
         add_vector(1, 0)
-        posb_tile(4, 2, 1)
-        make_posb(4)
+        add_vector(1, 1)
+        store(1)
+        quantise(1)
+        posb_tile(5, 2, 1)
         make_posb(5)
-        transposes(5)
+        make_posb(6)
         evacuate(4)
+        transposes(5)
         multiply(2, 0)
         multiply(2, 1)
         multiply(3, 0)
         reorder(6, 0)
         reorder(6, 1)
         evacuate(5)
-        add_vector(1, 1)
-        store(1)
         absmax(1, 0)
         absmax(1, 1)
         transposes(6)
         reorder(7, 0)
         reorder(7, 1)
-        quantise(2)
         add_vector(2, 0)
-        posb_tile(6, 2, 2)
-        make_posb(6)
+        add_vector(2, 1)
+        store(2)
+        quantise(2)
+        absmax(2, 0)
+        absmax(2, 1)
+        posb_tile(7, 1, 2)
         make_posb(7)
         evacuate(6)
         multiply(3, 1)
         transposes(7)
-        add_vector(2, 1)
-        store(2)
-        absmax(2, 0)
-        absmax(2, 1)
         evacuate(7)
         add_vector(3, 0)
+        add_vector(3, 1)
+        store(3)
         multiply(4, 0)
         multiply(4, 1)
         multiply(5, 0)
@@ -319,8 +325,6 @@ def tile_resampling_kernel(tc, encoded, W, b, pos_emb, out_0, out_1):
         add_gpsimd(4, 0)
         out_of_psum(4, 1)
         add_gpsimd(4, 1)
-        add_vector(3, 1)
-        store(3)
         store(4)
         absmax(3, 0)
         absmax(3, 1)

@@ -64,7 +64,7 @@ def tile_resampling_kernel(tc, encoded, W, b, pos_emb, out_0, out_1):
             for l in range(nl):
                 pos_sb[l0 + l] = pos_t[k][:, l, :]
         posb = {}
-        for l in (0, 1):
+        for l in (0, 1, 3, 4, 6):
             posb_v = const.tile([P, F], F32, name="posb%d" % l)
             posb[l] = posb_v[:]
         xr = {}
@@ -96,7 +96,7 @@ def tile_resampling_kernel(tc, encoded, W, b, pos_emb, out_0, out_1):
                 xc[u] = xc_t[g][:, k * 256:(k + 1) * 256]
                 xs[u] = xs_t[g][:, k * 256:(k + 1) * 256]
         for u in range(NU):
-            if u != 4:
+            if u not in (4,):
                 o_sb[u] = keep.tile([P, 2, F], F32, name="o%d" % u)
             q_sb[u] = keep.tile([P, 1024], FP8, name="q%d" % u)
         tp_of = {}
@@ -116,21 +116,23 @@ def tile_resampling_kernel(tc, encoded, W, b, pos_emb, out_0, out_1):
             i, l0 = UNITS[u]
             c = [i == ci and cl0 <= l0 < cl0 + nl for ci, cl0, nl in CHUNKS].index(True)
             cl0, nl = CHUNKS[c][1], CHUNKS[c][2]
-            v = xraw[c][:].bitcast(F32).rearrange("p a (l s ry h) -> p a l ry s h", l=nl, s=2, ry=8, h=8)
-            return v[:, :, l0 - cl0:l0 - cl0 + 2]
+            v = xraw[c][:].bitcast(F32).rearrange("p a (l s ry h w) -> p w a l ry s h", l=nl, s=2, ry=8, h=4, w=2)
+            return v[:, :, :, l0 - cl0:l0 - cl0 + 2]
 
         def reorder_first(k, copy):
-            copy(out=xr0[k][:].rearrange("p (a ry s h) -> p a ry s h", a=2, ry=8, s=2, h=8),
-                 in_=raw_words(0)[:, :, k])
+            dst = xr0[k][:].rearrange("p (w a ry s h) -> p w a ry s h", w=2, a=2, ry=8, s=2, h=4)
+            for w in range(2):
+                copy(out=dst[:, w], in_=raw_words(0)[:, w, :, k])
 
         def reorder(u, a):
-            dst = xr[u][:].rearrange("p l (a ry s h) -> p a l ry s h", a=2, ry=8, s=2, h=8)
-            nc.scalar.copy(out=dst[:, a], in_=raw_words(u)[:, a])
+            dst = xr[u][:].rearrange("p l (w a ry s h) -> p w a l ry s h", w=2, a=2, ry=8, s=2, h=4)
+            for w in range(2):
+                nc.scalar.copy(out=dst[:, w, a], in_=raw_words(u)[:, w, a])
 
         def transposes_first(k):
             tp = ps_t.tile([P, 2, 2, P], F32, name="tp")
             for w in range(2):
-                nc.tensor.transpose(out=tp[:, 0, w, :], in_=xr0[k][:, w:256:2], identity=ident[:])
+                nc.tensor.transpose(out=tp[:, 0, w, :], in_=xr0[k][:, w * P:(w + 1) * P], identity=ident[:])
             tp_of[0, k] = tp
 
         def evacuate_first(k):
@@ -144,7 +146,7 @@ def tile_resampling_kernel(tc, encoded, W, b, pos_emb, out_0, out_1):
             tp = ps_t.tile([P, 2, 2, P], F32, name="tp")
             for k in range(2):
                 for w in range(2):
-                    nc.tensor.transpose(out=tp[:, k, w, :], in_=xr[u][:, k, w:256:2], identity=ident[:])
+                    nc.tensor.transpose(out=tp[:, k, w, :], in_=xr[u][:, k, w * P:(w + 1) * P], identity=ident[:])
             tp_of[u] = tp
 
         def evacuate(u):
@@ -183,10 +185,16 @@ def tile_resampling_kernel(tc, encoded, W, b, pos_emb, out_0, out_1):
             nc.vector.tensor_reduce(out=stats[:, j:j + 1], in_=o_sb[u][:, k, :], axis=AX.X, op=ALU.max,
                                     apply_absolute_value=True)
 
-        def posb_tile(l, n, g):
-            t = keep.tile([P, n, F], F32, name="posb_%d" % l, tag="slot%d" % g, align_bytes=64)
-            for k in range(n):
-                posb[l + k] = t[:, k, :]
+        def posb_in_slot(l, g):
+            t = keep.tile([P, F], F32, name="posb%d" % l, tag="slot%d" % g, align_bytes=64)
+            posb[l] = t[:]
+
+        def o_in_slot(u, g):
+            o_sb[u] = keep.tile([P, 2, F], F32, name="o%d" % u, tag="slot%d" % g, align_bytes=64)
+
+        def store_tile(u, k):
+            i, l0 = UNITS[u]
+            nc.sync.dma_start(out=out_0[i].rearrange("(p l) f -> p l f", l=XL)[:, l0 + k:l0 + k + 1, :], in_=o_sb[u][:, k:k + 1, :])
 
         def make_posb_vector(l):
             nc.vector.tensor_tensor(out=posb[l], in0=pos_sb[l], in1=b_ps[:], op=ALU.add)
@@ -194,13 +202,14 @@ def tile_resampling_kernel(tc, encoded, W, b, pos_emb, out_0, out_1):
         def make_posb(l):
             nc.gpsimd.tensor_tensor(out=posb[l], in0=pos_sb[l], in1=b_all[:], op=ALU.add)
 
-        def cast(u, eng):
-            src = o_sb[u][:].rearrange("p l f -> p (l f)")
+        def cast(u, c0, n, eng):
+            src = o_sb[u][:].rearrange("p l f -> p (l f)")[:, c0:c0 + n]
+            dst = q_sb[u][:, c0:c0 + n]
             if eng == "v":
-                nc.vector.tensor_scalar(out=q_sb[u][:], in0=src, scalar1=fac[:, 0:1], scalar2=None,
+                nc.vector.tensor_scalar(out=dst, in0=src, scalar1=fac[:, 0:1], scalar2=None,
                                         op0=ALU.mult, saturate=False)
             else:
-                nc.scalar.activation(out=q_sb[u][:], in_=src, func=ACT.Identity, bias=zero[:, 0:1],
+                nc.scalar.activation(out=dst, in_=src, func=ACT.Identity, bias=zero[:, 0:1],
                                      scale=fac[:, 0:1], saturate=False)
 
         def store_bytes(u):
@@ -241,114 +250,114 @@ def tile_resampling_kernel(tc, encoded, W, b, pos_emb, out_0, out_1):
         reorder(1, 1)
         w_view = w_raw[:].rearrange("p j f -> p f j")
         nc.vector.tensor_copy(out=b_all[:], in_=b_ps[:])
-        nc.vector.tensor_copy(out=w_grp[:, 0:W_SPLIT, :], in_=w_view[:, 0:W_SPLIT, :])
         evacuate_first(0)
+        transposes(1)
+        nc.vector.tensor_copy(out=w_grp[:, 0:W_SPLIT, :], in_=w_view[:, 0:W_SPLIT, :])
         nc.scalar.copy(out=w_grp[:, W_SPLIT:F, :], in_=w_view[:, W_SPLIT:F, :])
         quantise_first(0)
         evacuate_first(1)
         nc.vector.quantize_mx(out=w_codes[:].bitcast(FP8X4), scales=w_scales[:], in_=w_grp[:].rearrange("p f j -> p (f j)"))
-        quantise_first(1)
-        make_posb_vector(0)
-        make_posb_vector(1)
-        transposes(1)
-        multiply(0, 0)
-        multiply(0, 1)
         evacuate(1)
+        multiply(0, 0)
+        quantise_first(1)
+        reorder(2, 0)
+        reorder(2, 1)
+        multiply(0, 1)
         quantise(0)
-        posb_tile(2, 1, 0)
-        for l in (3, 4):
-            posb_g = const.tile([P, F], F32, name="posb%d" % l)
-            posb[l] = posb_g[:]
+        posb_in_slot(2, 0)
         make_posb(2)
-        make_posb(3)
-        make_posb(4)
-        for u in (2, 3):
-            reorder(u, 0)
-            reorder(u, 1)
+        reorder(3, 0)
+        reorder(3, 1)
         transposes(2)
-        transposes(3)
-        multiply(1, 0)
-        multiply(1, 1)
+        make_posb_vector(0)
+        make_posb(3)
         evacuate(2)
+        transposes(3)
+        make_posb_vector(1)
+        make_posb(4)
+        evacuate(3)
+        multiply(1, 0)
         add_vector(0, 0)
+        reorder(4, 0)
+        reorder(4, 1)
+        multiply(1, 1)
         add_vector(0, 1)
+        reorder(5, 0)
+        reorder(5, 1)
+        transposes(4)
         store(0)
         absmax(0, 0)
-        absmax(0, 1)
-        evacuate(3)
-        for u in (4, 5):
-            reorder(u, 0)
-            reorder(u, 1)
-        transposes(4)
-        add_vector(1, 0)
-        add_vector(1, 1)
-        store(1)
-        quantise(1)
-        posb_tile(5, 2, 1)
-        make_posb(5)
-        make_posb(6)
         evacuate(4)
         transposes(5)
-        multiply(2, 0)
-        multiply(2, 1)
-        multiply(3, 0)
+        absmax(0, 1)
         reorder(6, 0)
         reorder(6, 1)
+        add_vector(1, 0)
         evacuate(5)
-        absmax(1, 0)
-        absmax(1, 1)
-        transposes(6)
+        add_vector(1, 1)
         reorder(7, 0)
         reorder(7, 1)
+        store(1)
+        quantise(1)
+        posb_in_slot(5, 1)
+        make_posb(5)
+        multiply(2, 0)
+        absmax(1, 0)
+        make_posb(6)
+        multiply(2, 1)
+        absmax(1, 1)
+        multiply(3, 0)
         add_vector(2, 0)
+        transposes(6)
         add_vector(2, 1)
-        store(2)
-        quantise(2)
-        absmax(2, 0)
-        absmax(2, 1)
-        posb_tile(7, 1, 2)
-        make_posb(7)
         evacuate(6)
         multiply(3, 1)
+        store(2)
+        quantise(2)
+        posb_in_slot(7, 2)
+        make_posb(7)
         transposes(7)
+        absmax(2, 0)
         evacuate(7)
-        add_vector(3, 0)
-        add_vector(3, 1)
-        store(3)
         multiply(4, 0)
-        multiply(4, 1)
-        multiply(5, 0)
-        multiply(5, 1)
-        quantise(3)
-        o_sb[4] = keep.tile([P, 2, F], F32, name="o4", tag="slot3", align_bytes=64)
+        absmax(2, 1)
         out_of_psum(4, 0)
-        add_gpsimd(4, 0)
+        multiply(4, 1)
+        add_vector(3, 0)
         out_of_psum(4, 1)
-        add_gpsimd(4, 1)
-        store(4)
-        absmax(3, 0)
-        absmax(3, 1)
+        multiply(5, 0)
+        add_vector(3, 1)
         out_of_psum(5, 0)
-        add_gpsimd(5, 0)
-        multiply(6, 0)
-        multiply(6, 1)
-        multiply(7, 0)
-        multiply(7, 1)
+        multiply(5, 1)
+        store(3)
+        quantise(3)
+        o_in_slot(4, 3)
+        add_gpsimd(4, 0)
         out_of_psum(5, 1)
-        add_gpsimd(5, 1)
+        multiply(6, 0)
+        absmax(3, 0)
+        add_gpsimd(4, 1)
         out_of_psum(6, 0)
-        add_gpsimd(6, 0)
-        absmax(4, 0)
+        multiply(6, 1)
+        store(4)
+        absmax(3, 1)
+        add_gpsimd(5, 0)
+        multiply(7, 0)
         add_vector(6, 1)
-        absmax(4, 1)
+        add_gpsimd(5, 1)
+        multiply(7, 1)
+        absmax(4, 0)
+        add_gpsimd(6, 0)
         add_vector(7, 0)
-        absmax(6, 1)
         add_vector(7, 1)
         store(7)
         store(5)
+        store(6)
+        absmax(6, 1)
+        absmax(4, 1)
         absmax(7, 0)
-        absmax(5, 0)
         absmax(7, 1)
+        absmax(5, 0)
         absmax(5, 1)
         n_early = n_stats[0] - 1
         nc.vector.tensor_reduce(out=pmax[:], in_=stats[:, 0:n_early], axis=AX.X, op=ALU.max)
@@ -356,24 +365,24 @@ def tile_resampling_kernel(tc, encoded, W, b, pos_emb, out_0, out_1):
         nc.tensor.transpose(out=am_ps[:, 0, :], in_=stats[:, n_early:n_early + 1].to_broadcast([P, P]), identity=ident[:])
         nc.tensor.transpose(out=am_ps[:, 1, :], in_=pmax[:, 0:1].to_broadcast([P, P]), identity=ident[:])
         absmax(6, 0)
-        store(6)
         nc.tensor.transpose(out=am_ps[:, 2, :], in_=stats[:, n_early + 1:n_early + 2].to_broadcast([P, P]), identity=ident[:])
         nc.vector.tensor_scalar(out=junk[:], in0=am_ps[:], scalar1=1.0 / 448.0, scalar2=None, op0=ALU.mult,
                                 op1=ALU.max, accum_out=scale[:, 0:1])
         nc.vector.reciprocal(out=fac[:], in_=scale[:])
-        cast(0, "v")
-        cast(2, "s")
-        cast(1, "v")
+        cast(0, 0, 1024, "v")
+        cast(2, 0, 1024, "s")
+        cast(1, 0, 1024, "v")
         store_bytes(0)
-        cast(3, "v")
+        cast(3, 0, 1024, "v")
         store_bytes(1)
-        cast(5, "s")
+        cast(5, 0, 1024, "s")
         store_bytes(2)
-        cast(4, "v")
+        cast(4, 0, 1024, "v")
         store_bytes(3)
-        cast(6, "v")
+        cast(6, 0, 1024, "v")
         store_bytes(4)
-        cast(7, "s")
+        cast(7, 0, 512, "s")
+        cast(7, 512, 512, "v")
         store_bytes(5)
         store_bytes(6)
         store_bytes(7)

@@ -96,7 +96,7 @@ def tile_resampling_kernel(tc, encoded, W, b, pos_emb, out_0, out_1):
                 xc[u] = xc_t[g][:, k * 256:(k + 1) * 256]
                 xs[u] = xs_t[g][:, k * 256:(k + 1) * 256]
         for u in range(NU):
-            if u not in (4,):
+            if u not in ():
                 o_sb[u] = keep.tile([P, 2, F], F32, name="o%d" % u)
             q_sb[u] = keep.tile([P, 1024], FP8, name="q%d" % u)
         tp_of = {}
@@ -124,10 +124,10 @@ def tile_resampling_kernel(tc, encoded, W, b, pos_emb, out_0, out_1):
             for w in range(2):
                 copy(out=dst[:, w], in_=raw_words(0)[:, w, :, k])
 
-        def reorder(u, a):
+        def reorder(u, a, copy=nc.scalar.copy):
             dst = xr[u][:].rearrange("p l (w a ry s h) -> p w a l ry s h", w=2, a=2, ry=8, s=2, h=4)
             for w in range(2):
-                nc.scalar.copy(out=dst[:, w, a], in_=raw_words(u)[:, w, a])
+                copy(out=dst[:, w, a], in_=raw_words(u)[:, w, a])
 
         def transposes_first(k):
             tp = ps_t.tile([P, 2, 2, P], F32, name="tp")
@@ -246,125 +246,125 @@ def tile_resampling_kernel(tc, encoded, W, b, pos_emb, out_0, out_1):
         nc.tensor.matmul(out=b_ps[:], lhsT=ones[:], rhs=b_row[:], start=True, stop=True)
         transposes_first(0)
         transposes_first(1)
-        reorder(1, 0)
-        reorder(1, 1)
         w_view = w_raw[:].rearrange("p j f -> p f j")
         nc.vector.tensor_copy(out=b_all[:], in_=b_ps[:])
+        reorder(1, 0)
+        reorder(1, 1)
+        nc.vector.tensor_copy(out=w_grp[:, 0:W_SPLIT, :], in_=w_view[:, 0:W_SPLIT, :])
         evacuate_first(0)
         transposes(1)
-        nc.vector.tensor_copy(out=w_grp[:, 0:W_SPLIT, :], in_=w_view[:, 0:W_SPLIT, :])
-        nc.scalar.copy(out=w_grp[:, W_SPLIT:F, :], in_=w_view[:, W_SPLIT:F, :])
         quantise_first(0)
-        evacuate_first(1)
+        nc.scalar.copy(out=w_grp[:, W_SPLIT:F, :], in_=w_view[:, W_SPLIT:F, :])
         nc.vector.quantize_mx(out=w_codes[:].bitcast(FP8X4), scales=w_scales[:], in_=w_grp[:].rearrange("p f j -> p (f j)"))
-        evacuate(1)
+        evacuate_first(1)
         multiply(0, 0)
         quantise_first(1)
-        reorder(2, 0)
-        reorder(2, 1)
+        evacuate(1)
         multiply(0, 1)
         quantise(0)
         posb_in_slot(2, 0)
         make_posb(2)
-        reorder(3, 0)
-        reorder(3, 1)
+        reorder(2, 0)
+        reorder(2, 1)
         transposes(2)
         make_posb_vector(0)
         make_posb(3)
-        evacuate(2)
+        reorder(3, 0)
+        reorder(3, 1)
         transposes(3)
         make_posb_vector(1)
         make_posb(4)
-        evacuate(3)
+        evacuate(2)
         multiply(1, 0)
         add_vector(0, 0)
         reorder(4, 0)
         reorder(4, 1)
         multiply(1, 1)
         add_vector(0, 1)
-        reorder(5, 0)
-        reorder(5, 1)
+        evacuate(3)
         transposes(4)
         store(0)
         absmax(0, 0)
-        evacuate(4)
+        reorder(5, 0)
+        reorder(5, 1)
         transposes(5)
         absmax(0, 1)
+        evacuate(4)
+        add_vector(1, 0)
         reorder(6, 0)
         reorder(6, 1)
-        add_vector(1, 0)
-        evacuate(5)
-        add_vector(1, 1)
-        reorder(7, 0)
-        reorder(7, 1)
-        store(1)
         quantise(1)
         posb_in_slot(5, 1)
         make_posb(5)
+        evacuate(5)
         multiply(2, 0)
-        absmax(1, 0)
+        add_vector(1, 1)
         make_posb(6)
+        reorder(7, 0)
+        reorder(7, 1)
         multiply(2, 1)
-        absmax(1, 1)
+        store(1)
+        absmax(1, 0)
         multiply(3, 0)
-        add_vector(2, 0)
+        absmax(1, 1)
         transposes(6)
-        add_vector(2, 1)
+        add_vector(2, 0)
         evacuate(6)
         multiply(3, 1)
+        add_vector(2, 1)
+        transposes(7)
         store(2)
         quantise(2)
         posb_in_slot(7, 2)
         make_posb(7)
-        transposes(7)
-        absmax(2, 0)
         evacuate(7)
         multiply(4, 0)
-        absmax(2, 1)
+        absmax(2, 0)
         out_of_psum(4, 0)
         multiply(4, 1)
-        add_vector(3, 0)
+        absmax(2, 1)
+        add_gpsimd(4, 0)
         out_of_psum(4, 1)
         multiply(5, 0)
-        add_vector(3, 1)
+        add_vector(3, 0)
+        add_gpsimd(4, 1)
         out_of_psum(5, 0)
         multiply(5, 1)
-        store(3)
         quantise(3)
-        o_in_slot(4, 3)
-        add_gpsimd(4, 0)
+        add_gpsimd(5, 0)
         out_of_psum(5, 1)
+        add_vector(3, 1)
+        add_gpsimd(5, 1)
         multiply(6, 0)
+        store(3)
+        store(4)
         absmax(3, 0)
-        add_gpsimd(4, 1)
         out_of_psum(6, 0)
         multiply(6, 1)
-        store(4)
         absmax(3, 1)
-        add_gpsimd(5, 0)
-        multiply(7, 0)
-        add_vector(6, 1)
-        add_gpsimd(5, 1)
-        multiply(7, 1)
-        absmax(4, 0)
         add_gpsimd(6, 0)
+        out_of_psum(6, 1)
+        multiply(7, 0)
+        absmax(4, 0)
+        add_gpsimd(6, 1)
+        multiply(7, 1)
         add_vector(7, 0)
         add_vector(7, 1)
         store(7)
         store(5)
         store(6)
-        absmax(6, 1)
         absmax(4, 1)
         absmax(7, 0)
         absmax(7, 1)
         absmax(5, 0)
         absmax(5, 1)
+        absmax(6, 0)
         n_early = n_stats[0] - 1
         nc.vector.tensor_reduce(out=pmax[:], in_=stats[:, 0:n_early], axis=AX.X, op=ALU.max)
         am_ps = ps_x.tile([P, 3, P], F32, name="am_ps", tag="misc")
         nc.tensor.transpose(out=am_ps[:, 0, :], in_=stats[:, n_early:n_early + 1].to_broadcast([P, P]), identity=ident[:])
         nc.tensor.transpose(out=am_ps[:, 1, :], in_=pmax[:, 0:1].to_broadcast([P, P]), identity=ident[:])
-        absmax(6, 0)
+        absmax(6, 1)
         nc.tensor.transpose(out=am_ps[:, 2, :], in_=stats[:, n_early + 1:n_early + 2].to_broadcast([P, P]), identity=ident[:])
         nc.vector.tensor_scalar(out=junk[:], in0=am_ps[:], scalar1=1.0 / 448.0, scalar2=None, op0=ALU.mult,
                                 op1=ALU.max, accum_out=scale[:, 0:1])

@@ -185,6 +185,12 @@ def tile_resampling_kernel(tc, encoded, W, b, pos_emb, out_0, out_1):
             nc.vector.tensor_reduce(out=stats[:, j:j + 1], in_=o_sb[u][:, k, :], axis=AX.X, op=ALU.max,
                                     apply_absolute_value=True)
 
+        def absmax_pair(u):
+            j = n_stats[0]
+            n_stats[0] = j + 1
+            nc.vector.tensor_reduce(out=stats[:, j:j + 1], in_=o_sb[u][:].rearrange("p l f -> p (l f)"), axis=AX.X,
+                                    op=ALU.max, apply_absolute_value=True)
+
         def posb_in_slot(l, g):
             t = keep.tile([P, F], F32, name="posb%d" % l, tag="slot%d" % g, align_bytes=64)
             posb[l] = t[:]
@@ -343,28 +349,27 @@ def tile_resampling_kernel(tc, encoded, W, b, pos_emb, out_0, out_1):
         multiply(6, 1)
         absmax(3, 1)
         add_gpsimd(6, 0)
-        out_of_psum(6, 1)
         multiply(7, 0)
-        absmax(4, 0)
-        add_gpsimd(6, 1)
+        add_vector(6, 1)
         multiply(7, 1)
+        absmax(4, 0)
         add_vector(7, 0)
         add_vector(7, 1)
         store(7)
         store(5)
         store(6)
+        absmax(6, 1)
         absmax(4, 1)
         absmax(7, 0)
         absmax(7, 1)
         absmax(5, 0)
         absmax(5, 1)
-        absmax(6, 0)
         n_early = n_stats[0] - 1
         nc.vector.tensor_reduce(out=pmax[:], in_=stats[:, 0:n_early], axis=AX.X, op=ALU.max)
         am_ps = ps_x.tile([P, 3, P], F32, name="am_ps", tag="misc")
         nc.tensor.transpose(out=am_ps[:, 0, :], in_=stats[:, n_early:n_early + 1].to_broadcast([P, P]), identity=ident[:])
         nc.tensor.transpose(out=am_ps[:, 1, :], in_=pmax[:, 0:1].to_broadcast([P, P]), identity=ident[:])
-        absmax(6, 1)
+        absmax(6, 0)
         nc.tensor.transpose(out=am_ps[:, 2, :], in_=stats[:, n_early + 1:n_early + 2].to_broadcast([P, P]), identity=ident[:])
         nc.vector.tensor_scalar(out=junk[:], in0=am_ps[:], scalar1=1.0 / 448.0, scalar2=None, op0=ALU.mult,
                                 op1=ALU.max, accum_out=scale[:, 0:1])

@@ -43,6 +43,7 @@ def tile_resampling_kernel(tc, encoded, W, b, pos_emb, out_0, out_1):
         ones = const.tile([P, P], BF16, name="ones")
         zero = const.tile([P, 1], F32, name="zero")
         ident = const.tile([P, P], F32, name="ident")
+        ident_b = const.tile([P, P], BF16, name="ident_b")
         warm = const.tile([P, 1], F32, name="warm")
         w_raw = const.tile([P, 4, F], BF16, name="w_raw")
         w_grp = const.tile([P, F, 4], BF16, name="w_grp", align_bytes=64)
@@ -76,8 +77,12 @@ def tile_resampling_kernel(tc, encoded, W, b, pos_emb, out_0, out_1):
             xg0.append(keep.tile([P, 512], BF16, name="xg0%d" % k, align_bytes=64))
             xc0.append(keep.tile([P, P], U32, name="xc0%d" % k, align_bytes=64))
             xs0.append(keep.tile([P, P], U8, name="xs0%d" % k, align_bytes=64))
-        for u in range(1, NU):
-            xr[u] = keep.tile([P, 2, 256], F32, name="xr%d" % u)
+        xr[1] = keep.tile([P, 2, 256], F32, name="xr1")
+        xr_pair = {}
+        for u in (2, 4, 6):
+            xr_pair[u] = keep.tile([P, 4, 256], F32, name="xr%d" % u)
+            xr[u] = xr_pair[u][:, 0:2, :]
+            xr[u + 1] = xr_pair[u][:, 2:4, :]
         xg = {}
         xc = {}
         xs = {}
@@ -125,9 +130,16 @@ def tile_resampling_kernel(tc, encoded, W, b, pos_emb, out_0, out_1):
                 copy(out=dst[:, w], in_=raw_words(0)[:, w, :, k])
 
         def reorder(u, a, copy=nc.scalar.copy):
-            dst = xr[u][:].rearrange("p l (w a ry s h) -> p w a l ry s h", w=2, a=2, ry=8, s=2, h=4)
+            dst = (xr[u] if u > 1 else xr[u][:]).rearrange("p l (w a ry s h) -> p w a l ry s h", w=2, a=2, ry=8, s=2, h=4)
             for w in range(2):
                 copy(out=dst[:, w, a], in_=raw_words(u)[:, w, a])
+
+        def reorder_pair(u):
+            src = xraw[u // 2][:].bitcast(F32).rearrange("p a (l s ry h w) -> p w a l ry s h", l=4, s=2, ry=8, h=4, w=2)
+            dst = xr_pair[u][:].rearrange("p l (w a ry s h) -> p w a l ry s h", w=2, a=2, ry=8, s=2, h=4)
+            for w in range(2):
+                for a in range(2):
+                    nc.scalar.copy(out=dst[:, w, a], in_=src[:, w, a])
 
         def transposes_first(k):
             tp = ps_t.tile([P, 2, 2, P], F32, name="tp")
@@ -174,6 +186,16 @@ def tile_resampling_kernel(tc, encoded, W, b, pos_emb, out_0, out_1):
 
         def add_gpsimd(u, k):
             nc.gpsimd.tensor_tensor(out=o_sb[u][:, k, :], in0=tmp_of[u, k][:], in1=posb[UNITS[u][1] + k], op=ALU.add)
+
+        def add_tensor(u, k):
+            total = ps_t.tile([P, F], F32, name="total", tag="tp")
+            nc.tensor.matmul(out=total[:], lhsT=ident_b[:], rhs=pos_sb[UNITS[u][1] + k], start=True, stop=False)
+            nc.tensor.matmul(out=total[:], lhsT=ones[:], rhs=b_row[:], start=False, stop=False)
+            nc.tensor.matmul(out=total[:], lhsT=ident[:], rhs=tmp_of[u, k][:], start=False, stop=True)
+            tp_of["sum", u, k] = total
+
+        def copy_sum(u, k):
+            nc.scalar.copy(out=o_sb[u][:, k, :], in_=tp_of["sum", u, k][:])
 
         def store(u):
             i, l0 = UNITS[u]
@@ -229,6 +251,7 @@ def tile_resampling_kernel(tc, encoded, W, b, pos_emb, out_0, out_1):
         load_chunk(0, 3, nc.scalar)
         nc.scalar.activation(out=warm[:], in_=zero[:], func=ACT.Identity, bias=zero[:, 0:1], scale=zero[:, 0:1])
         make_identity(nc, ident[:])
+        nc.gpsimd.tensor_copy(out=ident_b[:], in_=ident[:])
         load_chunk(0, 0, nc.sync)
         load_chunk(0, 1, nc.sync)
         load_chunk(0, 2, nc.sync)
@@ -353,17 +376,19 @@ def tile_resampling_kernel(tc, encoded, W, b, pos_emb, out_0, out_1):
         add_vector(6, 1)
         multiply(7, 1)
         absmax(4, 0)
+        out_of_psum(7, 1)
+        add_tensor(7, 1)
         add_vector(7, 0)
-        add_vector(7, 1)
+        copy_sum(7, 1)
         store(7)
         store(5)
         store(6)
         absmax(6, 1)
         absmax(4, 1)
         absmax(7, 0)
-        absmax(7, 1)
         absmax(5, 0)
         absmax(5, 1)
+        absmax(7, 1)
         n_early = n_stats[0] - 1
         nc.vector.tensor_reduce(out=pmax[:], in_=stats[:, 0:n_early], axis=AX.X, op=ALU.max)
         am_ps = ps_x.tile([P, 3, P], F32, name="am_ps", tag="misc")

from contextlib import ExitStack

import concourse.mybir as mybir
from concourse.masks import make_identity

F32 = mybir.dt.float32
BF16 = mybir.dt.bfloat16
U32 = mybir.dt.uint32
U8 = mybir.dt.uint8
FP8X4 = mybir.dt.float8_e4m3fn_x4
FP8 = mybir.dt.float8_e4m3fn
ALU = mybir.AluOpType
ACT = mybir.ActivationFunctionType
AX = mybir.AxisListType

P = 128
F = 512
XL = 8
FLOPS = 2 * 2048 * 512 * 512

POS_PIECES = [(0, 1), (1, 1), (2, 2), (4, 2), (6, 2)]
CHUNKS = [(0, 0, 4), (1, 0, 4), (0, 4, 4), (1, 4, 4)]
UNITS = [((u // 2) % 2, 4 * (u // 4) + 2 * (u % 2)) for u in range(8)]
NU = len(UNITS)
QGROUPS = [[1], [2, 3], [4, 5], [6, 7]]
W_SPLIT = 400


def tile_resampling_kernel(tc, encoded, W, b, pos_emb, out_0, out_1):
    nc = tc.nc
    with ExitStack() as ctx:
        const = ctx.enter_context(tc.tile_pool(name="const", bufs=1))
        keep = ctx.enter_context(tc.tile_pool(name="keep", bufs=1))
        ps_t = ctx.enter_context(tc.psum_pool(name="ps_t", bufs=2))
        ps_m = ctx.enter_context(tc.psum_pool(name="ps_m", bufs=5))
        ps_x = ctx.enter_context(tc.psum_pool(name="ps_x", bufs=1))
        ctx.enter_context(tc.manual_schedule())

        enc_v = encoded.rearrange("i (y a xh r) d -> i xh y a (r d)", y=32, a=2, xh=4, r=16)
        pos_v = pos_emb.rearrange("(p l) f -> p l f", l=XL)

        b_row = const.tile([P, F], BF16, name="b_row")
        ones = const.tile([P, P], BF16, name="ones")
        zero = const.tile([P, 1], F32, name="zero")
        ident = const.tile([P, P], F32, name="ident")
        ident_b = const.tile([P, P], BF16, name="ident_b")
        warm = const.tile([P, 1], F32, name="warm")
        w_raw = const.tile([P, 4, F], BF16, name="w_raw")
        w_grp = const.tile([P, F, 4], BF16, name="w_grp", align_bytes=64)
        w_codes = const.tile([P, F], U32, name="w_codes", align_bytes=64)
        w_scales = const.tile([P, F], U8, name="w_scales", align_bytes=64)
        b_all = const.tile([P, F], BF16, name="b_all")
        stats = const.tile([P, 16], F32, name="stats")
        pmax = const.tile([P, 1], F32, name="pmax")
        junk = const.tile([P, 3, P], F32, name="junk")
        scale = const.tile([P, 1], F32, name="scale")
        fac = const.tile([P, 1], F32, name="fac")
        xraw = []
        for c, (i, l0, nl) in enumerate(CHUNKS):
            xraw.append(keep.tile([P, 2, nl * 256], BF16, name="xraw%d" % c))
        pos_sb = {}
        pos_t = {}
        for k, (l0, nl) in enumerate(POS_PIECES):
            pos_t[k] = const.tile([P, nl, F], BF16, name="pos%d" % k)
            for l in range(nl):
                pos_sb[l0 + l] = pos_t[k][:, l, :]
        posb = {}
        for l in (0, 1, 3, 4, 6):
            posb_v = const.tile([P, F], F32, name="posb%d" % l)
            posb[l] = posb_v[:]
        xr = {}
        xr0 = [keep.tile([P, 256], F32, name="xr0a"), keep.tile([P, 256], F32, name="xr0b")]
        xc0 = []
        xs0 = []
        xg0 = []
        for k in range(2):
            xg0.append(keep.tile([P, 512], BF16, name="xg0%d" % k, align_bytes=64))
            xc0.append(keep.tile([P, P], U32, name="xc0%d" % k, align_bytes=64))
            xs0.append(keep.tile([P, P], U8, name="xs0%d" % k, align_bytes=64))
        xr[1] = keep.tile([P, 2, 256], F32, name="xr1")
        xr_pair = {}
        for u in (2, 4, 6):
            xr_pair[u] = keep.tile([P, 4, 256], F32, name="xr%d" % u)
            xr[u] = xr_pair[u][:, 0:2, :]
            xr[u + 1] = xr_pair[u][:, 2:4, :]
        xg = {}
        xc = {}
        xs = {}
        o_sb = {}
        q_sb = {}
        xg_t = {}
        xc_t = {}
        xs_t = {}
        for g, units in enumerate(QGROUPS):
            n = len(units)
            xg_t[g] = keep.tile([P, 1024 * n], BF16, name="xg%d" % g, tag="slot%d" % g, align_bytes=64)
            xc_t[g] = keep.tile([P, 256 * n], U32, name="xc%d" % g, align_bytes=64)
            xs_t[g] = keep.tile([P, 256 * n], U8, name="xs%d" % g, align_bytes=64)
            for k, u in enumerate(units):
                xg[u] = xg_t[g][:, k * 1024:(k + 1) * 1024]
                xc[u] = xc_t[g][:, k * 256:(k + 1) * 256]
                xs[u] = xs_t[g][:, k * 256:(k + 1) * 256]
        for u in range(NU):
            if u not in ():
                o_sb[u] = keep.tile([P, 2, F], F32, name="o%d" % u)
            q_sb[u] = keep.tile([P, 1024], FP8, name="q%d" % u)
        tp_of = {}
        acc_of = {}
        tmp_of = {}
        n_stats = [0]

        def load_chunk(c, xh, queue):
            i, l0, nl = CHUNKS[c]
            queue.dma_start(out=xraw[c][xh:P:4, :, :], in_=enc_v[i, xh, :, :, l0 * 256:(l0 + nl) * 256])

        def load_pos(k, queue):
            l0, nl = POS_PIECES[k]
            queue.dma_start(out=pos_t[k][:], in_=pos_v[:, l0:l0 + nl, :])

        def raw_words(u):
            i, l0 = UNITS[u]
            c = [i == ci and cl0 <= l0 < cl0 + nl for ci, cl0, nl in CHUNKS].index(True)
            cl0, nl = CHUNKS[c][1], CHUNKS[c][2]
            v = xraw[c][:].bitcast(F32).rearrange("p a (l s ry h w) -> p w a l ry s h", l=nl, s=2, ry=8, h=4, w=2)
            return v[:, :, :, l0 - cl0:l0 - cl0 + 2]

        def reorder_first(k, copy):
            dst = xr0[k][:].rearrange("p (w a ry s h) -> p w a ry s h", w=2, a=2, ry=8, s=2, h=4)
            for w in range(2):
                copy(out=dst[:, w], in_=raw_words(0)[:, w, :, k])

        def reorder(u, a, copy=nc.scalar.copy):
            dst = (xr[u] if u > 1 else xr[u][:]).rearrange("p l (w a ry s h) -> p w a l ry s h", w=2, a=2, ry=8, s=2, h=4)
            for w in range(2):
                copy(out=dst[:, w, a], in_=raw_words(u)[:, w, a])

        def reorder_pair(u):
            src = xraw[u // 2][:].bitcast(F32).rearrange("p a (l s ry h w) -> p w a l ry s h", l=4, s=2, ry=8, h=4, w=2)
            dst = xr_pair[u][:].rearrange("p l (w a ry s h) -> p w a l ry s h", w=2, a=2, ry=8, s=2, h=4)
            for w in range(2):
                for a in range(2):
                    nc.scalar.copy(out=dst[:, w, a], in_=src[:, w, a])

        def transposes_first(k):
            tp = ps_t.tile([P, 2, 2, P], F32, name="tp")
            for w in range(2):
                nc.tensor.transpose(out=tp[:, 0, w, :], in_=xr0[k][:, w * P:(w + 1) * P], identity=ident[:])
            tp_of[0, k] = tp

        def evacuate_first(k):
            nc.scalar.copy(out=xg0[k][:].bitcast(F32).rearrange("p (n w) -> p n w", w=2),
                           in_=tp_of[0, k][:, 0].rearrange("p w n -> p n w"))

        def quantise_first(k):
            nc.vector.quantize_mx(out=xc0[k][:].bitcast(FP8X4), scales=xs0[k][:], in_=xg0[k][:])

        def transposes(u):
            tp = ps_t.tile([P, 2, 2, P], F32, name="tp")
            for k in range(2):
                for w in range(2):
                    nc.tensor.transpose(out=tp[:, k, w, :], in_=xr[u][:, k, w * P:(w + 1) * P], identity=ident[:])
            tp_of[u] = tp

        def evacuate(u):
            nc.scalar.copy(out=xg[u].bitcast(F32).rearrange("p (k n w) -> p k n w", k=2, w=2),
                           in_=tp_of[u][:].rearrange("p k w n -> p k n w"))

        def quantise(g):
            nc.vector.quantize_mx(out=xc_t[g][:].bitcast(FP8X4), scales=xs_t[g][:], in_=xg_t[g][:])

        def multiply(u, k):
            acc = ps_m.tile([P, F], F32, name="acc")
            codes = xc0[k][:] if u == 0 else xc[u][:, k * P:(k + 1) * P]
            scales = xs0[k][:] if u == 0 else xs[u][:, k * P:(k + 1) * P]
            nc.tensor.matmul_mx(out=acc[:], lhsT=codes.bitcast(FP8X4), lhsT_scale=scales,
                                rhs=w_codes[:].bitcast(FP8X4), rhs_scale=w_scales[:], start=True, stop=True)
            acc_of[u, k] = acc

        def add_vector(u, k):
            nc.vector.tensor_tensor(out=o_sb[u][:, k, :], in0=acc_of[u, k][:], in1=posb[UNITS[u][1] + k], op=ALU.add)

        def out_of_psum(u, k):
            tmp = keep.tile([P, F], F32, name="tmp%d" % (2 * u + k))
            nc.scalar.copy(out=tmp[:], in_=acc_of[u, k][:])
            tmp_of[u, k] = tmp

        def add_gpsimd(u, k):
            nc.gpsimd.tensor_tensor(out=o_sb[u][:, k, :], in0=tmp_of[u, k][:], in1=posb[UNITS[u][1] + k], op=ALU.add)

        def add_tensor(u, k):
            total = ps_t.tile([P, F], F32, name="total", tag="tp")
            nc.tensor.matmul(out=total[:], lhsT=ident_b[:], rhs=pos_sb[UNITS[u][1] + k], start=True, stop=False)
            nc.tensor.matmul(out=total[:], lhsT=ones[:], rhs=b_row[:], start=False, stop=False)
            nc.tensor.matmul(out=total[:], lhsT=ident[:], rhs=tmp_of[u, k][:], start=False, stop=True)
            tp_of["sum", u, k] = total

        def copy_sum(u, k):
            nc.scalar.copy(out=o_sb[u][:, k, :], in_=tp_of["sum", u, k][:])

        def store(u):
            i, l0 = UNITS[u]
            nc.sync.dma_start(out=out_0[i].rearrange("(p l) f -> p l f", l=XL)[:, l0:l0 + 2, :], in_=o_sb[u][:])

        def absmax(u, k):
            j = n_stats[0]
            n_stats[0] = j + 1
            nc.vector.tensor_reduce(out=stats[:, j:j + 1], in_=o_sb[u][:, k, :], axis=AX.X, op=ALU.max,
                                    apply_absolute_value=True)

        def absmax_pair(u):
            j = n_stats[0]
            n_stats[0] = j + 1
            nc.vector.tensor_reduce(out=stats[:, j:j + 1], in_=o_sb[u][:].rearrange("p l f -> p (l f)"), axis=AX.X,
                                    op=ALU.max, apply_absolute_value=True)

        def posb_in_slot(l, g):
            t = keep.tile([P, F], F32, name="posb%d" % l, tag="slot%d" % g, align_bytes=64)
            posb[l] = t[:]

        def o_in_slot(u, g):
            o_sb[u] = keep.tile([P, 2, F], F32, name="o%d" % u, tag="slot%d" % g, align_bytes=64)

        def store_tile(u, k):
            i, l0 = UNITS[u]
            nc.sync.dma_start(out=out_0[i].rearrange("(p l) f -> p l f", l=XL)[:, l0 + k:l0 + k + 1, :], in_=o_sb[u][:, k:k + 1, :])

        def make_posb_vector(l):
            nc.vector.tensor_tensor(out=posb[l], in0=pos_sb[l], in1=b_ps[:], op=ALU.add)

        def make_posb(l):
            nc.gpsimd.tensor_tensor(out=posb[l], in0=pos_sb[l], in1=b_all[:], op=ALU.add)

        def cast(u, c0, n, eng):
            src = o_sb[u][:].rearrange("p l f -> p (l f)")[:, c0:c0 + n]
            dst = q_sb[u][:, c0:c0 + n]
            if eng == "v":
                nc.vector.tensor_scalar(out=dst, in0=src, scalar1=fac[:, 0:1], scalar2=None,
                                        op0=ALU.mult, saturate=False)
            else:
                nc.scalar.activation(out=dst, in_=src, func=ACT.Identity, bias=zero[:, 0:1],
                                     scale=fac[:, 0:1], saturate=False)

        def store_bytes(u):
            i, l0 = UNITS[u]
            nc.sync.dma_start(out=out_1[i].rearrange("(p l) f -> p (l f)", l=XL)[:, l0 * F:(l0 + 2) * F],
                              in_=q_sb[u][:].bitcast(U8))

        nc.gpsimd.memset(b_row[:], 0.0)
        nc.gpsimd.memset(ones[:], 1.0)
        nc.gpsimd.memset(zero[:], 0.0)
        load_chunk(0, 3, nc.scalar)
        nc.scalar.activation(out=warm[:], in_=zero[:], func=ACT.Identity, bias=zero[:, 0:1], scale=zero[:, 0:1])
        make_identity(nc, ident[:])
        nc.gpsimd.tensor_copy(out=ident_b[:], in_=ident[:])
        load_chunk(0, 0, nc.sync)
        load_chunk(0, 1, nc.sync)
        load_chunk(0, 2, nc.sync)
        nc.sync.dma_start(out=b_row[0:1, :], in_=b.rearrange("(o f) -> o f", o=1))
        nc.sync.dma_start(out=w_raw[:], in_=W.rearrange("(p j) f -> p j f", j=4))
        load_pos(0, nc.sync)
        for xh in range(4):
            load_chunk(1, xh, nc.sync)
        load_pos(1, nc.sync)
        load_pos(2, nc.sync)
        for xh in range(4):
            load_chunk(2, xh, nc.sync)
        load_pos(3, nc.sync)
        for xh in range(4):
            load_chunk(3, xh, nc.sync)
        load_pos(4, nc.sync)

        b_ps = ps_x.tile([P, F], F32, name="b_ps", tag="misc")
        reorder_first(0, nc.scalar.copy)
        reorder_first(1, nc.vector.tensor_copy)
        nc.tensor.matmul(out=b_ps[:], lhsT=ones[:], rhs=b_row[:], start=True, stop=True)
        transposes_first(0)
        transposes_first(1)
        w_view = w_raw[:].rearrange("p j f -> p f j")
        nc.vector.tensor_copy(out=b_all[:], in_=b_ps[:])
        reorder(1, 0)
        reorder(1, 1)
        nc.vector.tensor_copy(out=w_grp[:, 0:W_SPLIT, :], in_=w_view[:, 0:W_SPLIT, :])
        evacuate_first(0)
        transposes(1)
        quantise_first(0)
        nc.scalar.copy(out=w_grp[:, W_SPLIT:F, :], in_=w_view[:, W_SPLIT:F, :])
        nc.vector.quantize_mx(out=w_codes[:].bitcast(FP8X4), scales=w_scales[:], in_=w_grp[:].rearrange("p f j -> p (f j)"))
        evacuate_first(1)
        multiply(0, 0)
        quantise_first(1)
        evacuate(1)
        multiply(0, 1)
        quantise(0)
        posb_in_slot(2, 0)
        make_posb(2)
        reorder(2, 0)
        reorder(2, 1)
        transposes(2)
        make_posb_vector(0)
        make_posb(3)
        reorder(3, 0)
        reorder(3, 1)
        transposes(3)
        make_posb_vector(1)
        make_posb(4)
        evacuate(2)
        multiply(1, 0)
        add_vector(0, 0)
        reorder(4, 0)
        reorder(4, 1)
        multiply(1, 1)
        add_vector(0, 1)
        evacuate(3)
        transposes(4)
        store(0)
        absmax(0, 0)
        reorder(5, 0)
        reorder(5, 1)
        transposes(5)
        absmax(0, 1)
        evacuate(4)
        add_vector(1, 0)
        reorder(6, 0)
        reorder(6, 1)
        quantise(1)
        posb_in_slot(5, 1)
        make_posb(5)
        evacuate(5)
        multiply(2, 0)
        add_vector(1, 1)
        make_posb(6)
        reorder(7, 0)
        reorder(7, 1)
        multiply(2, 1)
        store(1)
        absmax(1, 0)
        multiply(3, 0)
        absmax(1, 1)
        transposes(6)
        add_vector(2, 0)
        evacuate(6)
        multiply(3, 1)
        add_vector(2, 1)
        transposes(7)
        store(2)
        quantise(2)
        posb_in_slot(7, 2)
        make_posb(7)
        evacuate(7)
        multiply(4, 0)
        absmax(2, 0)
        out_of_psum(4, 0)
        multiply(4, 1)
        absmax(2, 1)
        add_gpsimd(4, 0)
        out_of_psum(4, 1)
        multiply(5, 0)
        add_vector(3, 0)
        add_gpsimd(4, 1)
        out_of_psum(5, 0)
        multiply(5, 1)
        quantise(3)
        add_gpsimd(5, 0)
        out_of_psum(5, 1)
        add_vector(3, 1)
        add_gpsimd(5, 1)
        multiply(6, 0)
        store(3)
        store(4)
        absmax(3, 0)
        out_of_psum(6, 0)
        multiply(6, 1)
        absmax(3, 1)
        add_gpsimd(6, 0)
        multiply(7, 0)
        add_vector(6, 1)
        multiply(7, 1)
        absmax(4, 0)
        out_of_psum(7, 1)
        add_tensor(7, 1)
        add_vector(7, 0)
        copy_sum(7, 1)
        store(7)
        store(5)
        store(6)
        absmax(6, 1)
        absmax(4, 1)
        absmax(7, 0)
        absmax(5, 0)
        absmax(5, 1)
        absmax(7, 1)
        n_early = n_stats[0] - 1
        nc.vector.tensor_reduce(out=pmax[:], in_=stats[:, 0:n_early], axis=AX.X, op=ALU.max)
        am_ps = ps_x.tile([P, 3, P], F32, name="am_ps", tag="misc")
        nc.tensor.transpose(out=am_ps[:, 0, :], in_=stats[:, n_early:n_early + 1].to_broadcast([P, P]), identity=ident[:])
        nc.tensor.transpose(out=am_ps[:, 1, :], in_=pmax[:, 0:1].to_broadcast([P, P]), identity=ident[:])
        absmax(6, 0)
        nc.tensor.transpose(out=am_ps[:, 2, :], in_=stats[:, n_early + 1:n_early + 2].to_broadcast([P, P]), identity=ident[:])
        nc.vector.tensor_scalar(out=junk[:], in0=am_ps[:], scalar1=1.0 / 448.0, scalar2=None, op0=ALU.mult,
                                op1=ALU.max, accum_out=scale[:, 0:1])
        nc.vector.reciprocal(out=fac[:], in_=scale[:])
        cast(0, 0, 1024, "v")
        cast(2, 0, 1024, "s")
        cast(1, 0, 1024, "v")
        store_bytes(0)
        cast(3, 0, 1024, "v")
        store_bytes(1)
        cast(5, 0, 1024, "s")
        store_bytes(2)
        cast(4, 0, 1024, "v")
        store_bytes(3)
        cast(6, 0, 1024, "v")
        store_bytes(4)
        cast(7, 0, 512, "s")
        cast(7, 512, 512, "v")
        store_bytes(5)
        store_bytes(6)
        store_bytes(7)
